import numpy as np
import ml_dtypes


def mxq(x, axis, fmt="e4m3"):
    dtype, down = {"e4m3": (ml_dtypes.float8_e4m3fn, 7), "e5m2": (ml_dtypes.float8_e5m2, 14)}[fmt]
    v = np.moveaxis(np.asarray(x, np.float32).astype(ml_dtypes.bfloat16).astype(np.float64), axis, -1)
    blocks = v.reshape(v.shape[:-1] + (-1, 32))
    amax = np.abs(blocks).max(-1, keepdims=True)
    byte = np.maximum(np.where(amax > 0, np.frexp(amax)[1] - 1 + 127, 0) - down, 1)
    scale = np.exp2(byte - 127.0)
    codes = (blocks / scale).astype(np.float32).astype(dtype).astype(np.float64)
    return np.moveaxis((codes * scale).reshape(v.shape), -1, axis)


WIDE = False


def mx_kscale(k):
    if not WIDE:
        return np.ones(k)
    levels = np.array([10, -10, 5, -5, 0])
    a = np.random.permutation(np.resize(levels, k // 512 * 4)).reshape(k // 512, 4)
    idx = np.arange(k)
    return np.exp2(a[idx // 512, idx % 128 // 32])


BF16 = ml_dtypes.bfloat16


def bf(x):
    return np.asarray(x, np.float32).astype(BF16)


def f64(x):
    return np.asarray(x).astype(np.float64)


B, N, C, H, W, R = 4096, 1024, 128, 2, 2, 4
D = C * H * W
PI_2 = 3.14159 / 2
EPS = 1e-8
RHO = 0.85


def unit_rows(v):
    return v / np.sqrt((v * v).sum(-1, keepdims=True))


def setup_inputs():
    p = np.random.standard_normal((R, D))
    k = np.sqrt(RHO) * unit_rows(np.random.standard_normal((B, R))) @ p + np.sqrt(1.0 - RHO) * np.random.standard_normal((B, D))
    m = np.sqrt(RHO) * unit_rows(np.random.standard_normal((N, R))) @ p + np.sqrt(1.0 - RHO) * np.random.standard_normal((N, D))
    g = mx_kscale(D)[np.random.randint(0, D, B)]
    k = k * np.exp(0.3 * np.random.standard_normal((B, 1))) * g[:, None]
    m = m * np.exp(0.3 * np.random.standard_normal((N, 1)))
    return {"key": bf(k.reshape(B, C, H, W)), "memory": bf(m.reshape(N, C, H, W))}


def reference(key, memory):
    k = f64(key).reshape(B, -1)
    m = f64(memory).reshape(N, -1)
    dots = mxq(k, 1, "e4m3") @ mxq(m, 1, "e4m3").T
    k_norm = np.maximum(np.sqrt((k * k).sum(-1, keepdims=True)), EPS)
    m_norm = np.maximum(np.sqrt((m * m).sum(-1)), EPS)
    cos = dots / (k_norm * m_norm[None, :])
    t = np.tan(cos * PI_2)
    e = np.exp(t - t.max(1, keepdims=True))
    w = e / e.sum(1, keepdims=True)
    out = mxq(w, 1, "e4m3") @ mxq(m, 0, "e4m3")
    return out.reshape(B, C, H, W)

@@ -1,0 +1,351 @@
+from contextlib import ExitStack
+
+import concourse.mybir as mybir
+from concourse.masks import make_identity
+
+F32 = mybir.dt.float32
+BF16 = mybir.dt.bfloat16
+U32 = mybir.dt.uint32
+U8 = mybir.dt.uint8
+FP8X4 = mybir.dt.float8_e4m3fn_x4
+ACT = mybir.ActivationFunctionType
+ALU = mybir.AluOpType
+AXIS = mybir.AxisListType
+
+P = 128
+PACK = 4
+B, N, D = 4096, 1024, 512
+TILES = B // P
+GROUP = 8
+GROUPS = TILES // GROUP
+N_BLOCKS = N // P
+N_PASSES = N // (P * PACK)
+BANK = 512
+HALVES = N // BANK
+PI_2 = 3.14159 / 2
+EPS = 1e-8
+HUGE = 3.0e38
+EXP_LAG = 4
+
+FLOPS = 2 * B * N * D * 2
+
+
+def tile_memory_t_kernel(tc, key, memory, out):
+    nc = tc.nc
+    key_rows = key.rearrange("(p i) c h w -> p i (c h w)", i=TILES)
+    out_rows = out.rearrange("(p i) c h w -> p i (c h w)", i=TILES)
+    mem_rows = memory.rearrange("(c p t) a h w -> p c t (a h w)", c=N_PASSES, t=PACK)
+
+    with ExitStack() as stack:
+        stack.enter_context(tc.manual_schedule())
+        keep = stack.enter_context(tc.tile_pool(name="keep", bufs=1))
+        k_pool = stack.enter_context(tc.tile_pool(name="k_pool", bufs=2))
+        stat = stack.enter_context(tc.tile_pool(name="stat", bufs=2))
+        a_pool = stack.enter_context(tc.tile_pool(name="a_pool", bufs=GROUP + 4))
+        b_pool = stack.enter_context(tc.tile_pool(name="b_pool", bufs=GROUP))
+        w_pool = stack.enter_context(tc.tile_pool(name="w_pool", bufs=GROUP + 2))
+        post = stack.enter_context(tc.tile_pool(name="post", bufs=3))
+        dots_psum = stack.enter_context(tc.psum_pool(name="dots_psum", bufs=4))
+        turn_psum = stack.enter_context(tc.psum_pool(name="turn_psum", bufs=3))
+        out_psum = stack.enter_context(tc.psum_pool(name="out_psum", bufs=1))
+
+        def inverse_norm(sum_sq, width, factor, name):
+            rough = stat.tile([P, width], F32, name=name + "_rough")
+            nc.scalar.activation(out=rough[:], in_=sum_sq[:], func=ACT.Abs_reciprocal_sqrt)
+            nc.vector.tensor_scalar_min(out=rough[:], in0=rough[:], scalar1=1.0 / EPS)
+            step = stat.tile([P, width], F32, name=name + "_step")
+            nc.vector.tensor_tensor(out=step[:], in0=sum_sq[:], in1=rough[:], op=ALU.mult)
+            nc.vector.tensor_tensor(out=step[:], in0=step[:], in1=rough[:], op=ALU.mult)
+            nc.vector.tensor_scalar(
+                out=step[:], in0=step[:], scalar1=-0.5, scalar2=1.5, op0=ALU.mult, op1=ALU.add
+            )
+            fine = stat.tile([P, width], F32, name=name + "_fine")
+            nc.vector.tensor_tensor(out=fine[:], in0=rough[:], in1=step[:], op=ALU.mult)
+            nc.vector.tensor_scalar(
+                out=fine[:], in0=fine[:], scalar1=1.0 / EPS, scalar2=factor, op0=ALU.min, op1=ALU.mult
+            )
+            return fine
+
+        def turn_words(rows_sb, grouped, first, count):
+            words = rows_sb.bitcast(F32)
+            turned = turn_psum.tile([P, count, 2, P], F32, name="turned", tag="turn")
+            for a in range(count):
+                for u in range(2):
+                    nc.tensor.transpose(
+                        out=turned[:, a, u, :],
+                        in_=words[:, first + a, u * P : (u + 1) * P],
+                        identity=ident_f32[:],
+                    )
+            nc.vector.tensor_copy(
+                out=grouped.bitcast(F32)[:, first : first + count, :, :],
+                in_=turned[:].rearrange("p a u r -> p a r u"),
+            )
+
+        one = keep.tile([P, 1], F32, name="one")
+        nc.vector.memset(one[:], 1.0)
+        nc.scalar.activation(out=one[:], in_=one[:], func=ACT.Abs_reciprocal_sqrt)
+
+        m_sb = keep.tile([P, N_BLOCKS, D], BF16, name="m_sb")
+        nc.sync.dma_start(
+            out=m_sb[:].rearrange("p (c t) d -> p c t d", c=N_PASSES), in_=mem_rows
+        )
+        k_sb = {}
+
+        def load_k(g):
+            k_sb[g] = k_pool.tile([P, GROUP, D], BF16, name="k_sb")
+            nc.sync.dma_start(out=k_sb[g][:], in_=key_rows[:, g * GROUP : (g + 1) * GROUP, :])
+
+        load_k(0)
+        load_k(1)
+
+        ident_f32 = keep.tile([P, P], F32, name="ident_f32")
+        make_identity(nc, ident_f32[:])
+        ident_bf16 = keep.tile([P, P], BF16, name="ident_bf16")
+        make_identity(nc, ident_bf16[:])
+
+        squares = keep.tile([P, GROUP, D], BF16, name="squares")
+
+        def sum_squares(rows_sb, sum_sq, j):
+            nc.scalar.activation(
+                out=squares[:, j, :], in_=rows_sb[:, j, :], func=ACT.Square, accum_out=sum_sq[:, j : j + 1]
+            )
+
+        m_sum_sq = keep.tile([P, N_BLOCKS], F32, name="m_sum_sq")
+        for j in range(N_BLOCKS):
+            sum_squares(m_sb, m_sum_sq, j)
+
+        m1_grouped = keep.tile([P, N_BLOCKS, P, PACK], BF16, name="m1_grouped", align_bytes=64)
+        for j in range(0, N_BLOCKS, 2):
+            turn_words(m_sb[:], m1_grouped[:], j, 2)
+        m1_codes = keep.tile([P, N], U32, name="m1_codes", align_bytes=64)
+        m1_scales = keep.tile([P, N], U8, name="m1_scales", align_bytes=64)
+        nc.vector.quantize_mx(
+            out=m1_codes[:].bitcast(FP8X4),
+            scales=m1_scales[:],
+            in_=m1_grouped[:].rearrange("p j r t -> p (j r t)"),
+        )
+
+        m_inv = inverse_norm(m_sum_sq, N_BLOCKS, 1.0, "m_inv")
+        m_inv_all = keep.tile([P, N], F32, name="m_inv_all")
+        for h in range(HALVES):
+            spread = dots_psum.tile([P, BANK], F32, name="spread", tag="dots")
+            for a in range(BANK // P):
+                j = h * (BANK // P) + a
+                nc.tensor.matmul(
+                    out=spread[:, a * P : (a + 1) * P],
+                    lhsT=m_inv[:, j : j + 1].to_broadcast([P, P]),
+                    rhs=ident_f32[:],
+                    start=True,
+                    stop=True,
+                )
+            nc.vector.tensor_copy(out=m_inv_all[:, h * BANK : (h + 1) * BANK], in_=spread[:])
+
+        m2_grouped = keep.tile([P, N_PASSES, D, PACK], BF16, name="m2_grouped", align_bytes=64)
+        for c in range(N_PASSES):
+            nc.gpsimd.tensor_scalar(
+                out=m2_grouped[:, c, :, :],
+                in0=m_sb[:, c * PACK : (c + 1) * PACK, :].rearrange("p t d -> p d t"),
+                scalar1=1.0,
+                scalar2=0.0,
+                op0=ALU.mult,
+                op1=ALU.add,
+            )
+        m2_codes = keep.tile([P, N_PASSES * D], U32, name="m2_codes", align_bytes=64)
+        m2_scales = keep.tile([P, N_PASSES * D], U8, name="m2_scales", align_bytes=64)
+
+        k_sum_sq = {}
+        k_scale = {}
+        k_codes = {}
+        k_scales = {}
+
+        def quantise_k(g):
+            k_grouped = k_pool.tile([P, GROUP, P, PACK], BF16, name="k_grouped", bufs=1, align_bytes=64)
+            for j in range(0, GROUP, 2):
+                turn_words(k_sb[g][:], k_grouped[:], j, 2)
+            k_codes[g] = k_pool.tile([P, GROUP * P], U32, name="k_codes", align_bytes=64)
+            k_scales[g] = k_pool.tile([P, GROUP * P], U8, name="k_scales", align_bytes=64)
+            nc.vector.quantize_mx(
+                out=k_codes[g][:].bitcast(FP8X4),
+                scales=k_scales[g][:],
+                in_=k_grouped[:].rearrange("p j r t -> p (j r t)"),
+            )
+
+        k_sum_sq[0] = stat.tile([P, GROUP], F32, name="k_sum_sq")
+        for j in range(GROUP):
+            sum_squares(k_sb[0], k_sum_sq[0], j)
+        quantise_k(0)
+        k_scale[0] = inverse_norm(k_sum_sq[0], GROUP, PI_2, "k_inv")
+
+        dots = {}
+        a_tiles = {}
+        b_tiles = {}
+        neg_max = {}
+        sums = {}
+        inv_sums = {}
+        w_tiles = {}
+        w_turned = {}
+        w_grouped = {}
+        w_codes = {}
+        w_scales = {}
+        out_acc = {}
+
+        def first_matmul(i):
+            g, j = divmod(i, GROUP)
+            for h in range(HALVES):
+                dots[i, h] = dots_psum.tile([P, BANK], F32, name="dots", tag="dots")
+                nc.tensor.matmul_mx(
+                    out=dots[i, h][:],
+                    lhsT=k_codes[g][:, j * P : (j + 1) * P].bitcast(FP8X4),
+                    lhsT_scale=k_scales[g][:, j * P : (j + 1) * P],
+                    rhs=m1_codes[:, h * BANK : (h + 1) * BANK].bitcast(FP8X4),
+                    rhs_scale=m1_scales[:, h * BANK : (h + 1) * BANK],
+                    start=True,
+                    stop=True,
+                )
+
+        def sine(i):
+            g, j = divmod(i, GROUP)
+            a_tiles[i] = a_pool.tile([P, N], F32, name="a_tile")
+            for h in range(HALVES):
+                nc.vector.tensor_tensor(
+                    out=a_tiles[i][:, h * BANK : (h + 1) * BANK],
+                    in0=dots[i, h][:],
+                    in1=m_inv_all[:, h * BANK : (h + 1) * BANK],
+                    op=ALU.mult,
+                )
+            nc.scalar.activation(
+                out=a_tiles[i][:], in_=a_tiles[i][:], func=ACT.Sin, scale=k_scale[g][:, j : j + 1]
+            )
+            b_tiles[i] = b_pool.tile([P, N], F32, name="b_tile")
+            nc.gpsimd.tensor_tensor(out=b_tiles[i][:], in0=a_tiles[i][:], in1=a_tiles[i][:], op=ALU.mult)
+
+        def inverse_cosine(i):
+            nc.scalar.activation(
+                out=b_tiles[i][:], in_=b_tiles[i][:], func=ACT.Abs_reciprocal_sqrt, scale=-1.0, bias=1.0
+            )
+
+        def tangent_and_max(i):
+            g, j = divmod(i, GROUP)
+            nc.vector.scalar_tensor_tensor(
+                out=a_tiles[i][:], in0=b_tiles[i][:], scalar=HUGE, in1=a_tiles[i][:], op0=ALU.min, op1=ALU.mult
+            )
+            nc.vector.tensor_reduce(
+                out=neg_max[g][:, j : j + 1], in_=a_tiles[i][:], axis=AXIS.X, op=ALU.max, negate=True
+            )
+
+        def softmax(i):
+            g, j = divmod(i, GROUP)
+            nc.scalar.activation(
+                out=a_tiles[i][:],
+                in_=a_tiles[i][:],
+                func=ACT.Exp,
+                bias=neg_max[g][:, j : j + 1],
+                accum_out=sums[g][:, j : j + 1],
+            )
+            nc.vector.reciprocal(out=inv_sums[g][:, j : j + 1], in_=sums[g][:, j : j + 1])
+            w_tiles[i] = w_pool.tile([P, N], BF16, name="w_tile")
+            nc.gpsimd.tensor_scalar(
+                out=w_tiles[i][:],
+                in0=a_tiles[i][:],
+                scalar1=inv_sums[g][:, j : j + 1],
+                scalar2=0.0,
+                op0=ALU.mult,
+                op1=ALU.add,
+            )
+
+        def turn_w(i):
+            w_turned[i] = turn_psum.tile([P, N_BLOCKS, P], BF16, name="w_turned", tag="turn")
+            for f in range(N_BLOCKS):
+                nc.tensor.transpose(
+                    out=w_turned[i][:, f, :], in_=w_tiles[i][:, f * P : (f + 1) * P], identity=ident_bf16[:]
+                )
+
+        def group_w(i):
+            w_grouped[i] = post.tile([P, N_PASSES, P, PACK], BF16, name="w_grouped", align_bytes=64)
+            nc.vector.tensor_copy(
+                out=w_grouped[i][:], in_=w_turned[i][:].rearrange("p (c t) r -> p c r t", c=N_PASSES)
+            )
+
+        def second_matmul(i):
+            w_codes[i] = post.tile([P, N_PASSES * P], U32, name="w_codes", align_bytes=64)
+            w_scales[i] = post.tile([P, N_PASSES * P], U8, name="w_scales", align_bytes=64)
+            nc.vector.quantize_mx(
+                out=w_codes[i][:].bitcast(FP8X4),
+                scales=w_scales[i][:],
+                in_=w_grouped[i][:].rearrange("p c r t -> p (c r t)"),
+            )
+            out_acc[i] = out_psum.tile([P, D], F32, name="out_acc")
+            for c in range(N_PASSES):
+                nc.tensor.matmul_mx(
+                    out=out_acc[i][:],
+                    lhsT=w_codes[i][:, c * P : (c + 1) * P].bitcast(FP8X4),
+                    lhsT_scale=w_scales[i][:, c * P : (c + 1) * P],
+                    rhs=m2_codes[:, c * D : (c + 1) * D].bitcast(FP8X4),
+                    rhs_scale=m2_scales[:, c * D : (c + 1) * D],
+                    start=(c == 0),
+                    stop=(c == N_PASSES - 1),
+                )
+
+        def store(i):
+            out_sb = post.tile([P, D], F32, name="out_sb")
+            nc.scalar.copy(out=out_sb[:], in_=out_acc[i][:])
+            nc.sync.dma_start(out=out_rows[:, i, :], in_=out_sb[:])
+
+        def finish_step(s, lo, hi):
+            if lo <= s + 1 < hi:
+                turn_w(s + 1)
+            if lo <= s - 2 < hi:
+                store(s - 2)
+            if lo <= s < hi:
+                group_w(s)
+            if lo <= s - 1 < hi:
+                second_matmul(s - 1)
+
+        first_matmul(0)
+        for g in range(GROUPS + 1):
+            here = g * GROUP
+            lo, hi = here - GROUP, here
+            if g + 2 < GROUPS:
+                load_k(g + 2)
+            if g + 1 < GROUPS:
+                k_sum_sq[g + 1] = stat.tile([P, GROUP], F32, name="k_sum_sq")
+
+            for j in range(GROUP):
+                if g < GROUPS:
+                    if j + 1 < GROUP:
+                        first_matmul(here + j + 1)
+                    sine(here + j)
+                if g > 0:
+                    finish_step(lo + j, lo, hi)
+                if g + 1 < GROUPS:
+                    sum_squares(k_sb[g + 1], k_sum_sq[g + 1], j)
+            if g == 0:
+                nc.vector.quantize_mx(
+                    out=m2_codes[:].bitcast(FP8X4),
+                    scales=m2_scales[:],
+                    in_=m2_grouped[:].rearrange("p c d t -> p (c d t)"),
+                )
+            else:
+                finish_step(hi, lo, hi)
+                finish_step(hi + 1, lo, hi)
+            if g == GROUPS:
+                break
+
+            if g + 1 < GROUPS:
+                k_scale[g + 1] = inverse_norm(k_sum_sq[g + 1], GROUP, PI_2, "k_inv")
+            for j in range(GROUP):
+                inverse_cosine(here + j)
+
+            neg_max[g] = stat.tile([P, GROUP], F32, name="neg_max")
+            sums[g] = stat.tile([P, GROUP], F32, name="sums")
+            inv_sums[g] = stat.tile([P, GROUP], F32, name="inv_sums")
+            for j in range(GROUP + EXP_LAG):
+                if j < GROUP:
+                    tangent_and_max(here + j)
+                if j >= EXP_LAG:
+                    softmax(here + j - EXP_LAG)
+
+            if g + 1 < GROUPS:
+                quantise_k(g + 1)
+                first_matmul(here + GROUP)
+            turn_w(here)

@@ -14,18 +14,20 @@ AXIS = mybir.AxisListType
 
 P = 128
 PACK = 4
+K_PASS = P * PACK
 B, N, D = 4096, 1024, 512
 TILES = B // P
 GROUP = 8
 GROUPS = TILES // GROUP
 N_BLOCKS = N // P
-N_PASSES = N // (P * PACK)
+N_PASSES = N // K_PASS
 BANK = 512
 HALVES = N // BANK
+DOTS_TILES = 2
+EXP_LAG = 4
 PI_2 = 3.14159 / 2
 EPS = 1e-8
 HUGE = 3.0e38
-EXP_LAG = 4
 
 FLOPS = 2 * B * N * D * 2
 
@@ -43,11 +45,10 @@ def tile_memory_t_kernel(tc, key, memory, out):
         stat = stack.enter_context(tc.tile_pool(name="stat", bufs=2))
         a_pool = stack.enter_context(tc.tile_pool(name="a_pool", bufs=GROUP + 4))
         b_pool = stack.enter_context(tc.tile_pool(name="b_pool", bufs=GROUP))
-        w_pool = stack.enter_context(tc.tile_pool(name="w_pool", bufs=GROUP + 2))
-        post = stack.enter_context(tc.tile_pool(name="post", bufs=3))
-        dots_psum = stack.enter_context(tc.psum_pool(name="dots_psum", bufs=4))
-        turn_psum = stack.enter_context(tc.psum_pool(name="turn_psum", bufs=3))
-        out_psum = stack.enter_context(tc.psum_pool(name="out_psum", bufs=1))
+        w_pool = stack.enter_context(tc.tile_pool(name="w_pool", bufs=GROUP + 1))
+        short = stack.enter_context(tc.tile_pool(name="short", bufs=3))
+        banks = stack.enter_context(tc.psum_pool(name="banks", bufs=6))
+        out_psum = stack.enter_context(tc.psum_pool(name="out_psum", bufs=2))
 
         def inverse_norm(sum_sq, width, factor, name):
             rough = stat.tile([P, width], F32, name=name + "_rough")
@@ -66,29 +67,22 @@ def tile_memory_t_kernel(tc, key, memory, out):
             )
             return fine
 
-        def turn_words(rows_sb, grouped, first, count):
-            words = rows_sb.bitcast(F32)
-            turned = turn_psum.tile([P, count, 2, P], F32, name="turned", tag="turn")
-            for a in range(count):
+        def turn_words(rows):
+            words = rows.bitcast(F32)
+            turned = banks.tile([P, 2, 2, P], F32, name="turned", tag="bank")
+            for a in range(2):
                 for u in range(2):
                     nc.tensor.transpose(
-                        out=turned[:, a, u, :],
-                        in_=words[:, first + a, u * P : (u + 1) * P],
-                        identity=ident_f32[:],
+                        out=turned[:, a, u, :], in_=words[:, a, u * P : (u + 1) * P], identity=ident_f32[:]
                     )
-            nc.vector.tensor_copy(
-                out=grouped.bitcast(F32)[:, first : first + count, :, :],
-                in_=turned[:].rearrange("p a u r -> p a r u"),
-            )
+            return turned
 
         one = keep.tile([P, 1], F32, name="one")
         nc.vector.memset(one[:], 1.0)
         nc.scalar.activation(out=one[:], in_=one[:], func=ACT.Abs_reciprocal_sqrt)
 
         m_sb = keep.tile([P, N_BLOCKS, D], BF16, name="m_sb")
-        nc.sync.dma_start(
-            out=m_sb[:].rearrange("p (c t) d -> p c t d", c=N_PASSES), in_=mem_rows
-        )
+        nc.sync.dma_start(out=m_sb[:].rearrange("p (c t) d -> p c t d", c=N_PASSES), in_=mem_rows)
         k_sb = {}
 
         def load_k(g):
@@ -100,8 +94,6 @@ def tile_memory_t_kernel(tc, key, memory, out):
 
         ident_f32 = keep.tile([P, P], F32, name="ident_f32")
         make_identity(nc, ident_f32[:])
-        ident_bf16 = keep.tile([P, P], BF16, name="ident_bf16")
-        make_identity(nc, ident_bf16[:])
 
         squares = keep.tile([P, GROUP, D], BF16, name="squares")
 
@@ -110,25 +102,49 @@ def tile_memory_t_kernel(tc, key, memory, out):
                 out=squares[:, j, :], in_=rows_sb[:, j, :], func=ACT.Square, accum_out=sum_sq[:, j : j + 1]
             )
 
+        k_sum_sq = {}
+        k_scale = {}
+        k_codes = {}
+        k_scales = {}
+
+        def quantise_k(g):
+            k_grouped = k_pool.tile([P, GROUP, P, PACK], BF16, name="k_grouped", bufs=1, align_bytes=64)
+            for j in range(0, GROUP, 2):
+                turned = turn_words(k_sb[g][:, j : j + 2, :])
+                nc.vector.tensor_copy(
+                    out=k_grouped[:, j : j + 2, :, :].bitcast(F32), in_=turned[:].rearrange("p a u r -> p a r u")
+                )
+            k_codes[g] = k_pool.tile([P, GROUP * P], U32, name="k_codes", align_bytes=64)
+            k_scales[g] = k_pool.tile([P, GROUP * P], U8, name="k_scales", align_bytes=64)
+            nc.vector.quantize_mx(
+                out=k_codes[g][:].bitcast(FP8X4),
+                scales=k_scales[g][:],
+                in_=k_grouped[:].rearrange("p j r t -> p (j r t)"),
+            )
+
         m_sum_sq = keep.tile([P, N_BLOCKS], F32, name="m_sum_sq")
         for j in range(N_BLOCKS):
             sum_squares(m_sb, m_sum_sq, j)
 
-        m1_grouped = keep.tile([P, N_BLOCKS, P, PACK], BF16, name="m1_grouped", align_bytes=64)
-        for j in range(0, N_BLOCKS, 2):
-            turn_words(m_sb[:], m1_grouped[:], j, 2)
+        m1_grouped = keep.tile([P, N_BLOCKS // 2, P, 2, PACK], BF16, name="m1_grouped", align_bytes=64)
+        for v in range(N_BLOCKS // 2):
+            turned = turn_words(m_sb[:, 2 * v : 2 * v + 2, :])
+            nc.vector.tensor_copy(
+                out=m1_grouped[:, v, :, :, :].bitcast(F32), in_=turned[:].rearrange("p e u r -> p r e u")
+            )
         m1_codes = keep.tile([P, N], U32, name="m1_codes", align_bytes=64)
         m1_scales = keep.tile([P, N], U8, name="m1_scales", align_bytes=64)
         nc.vector.quantize_mx(
             out=m1_codes[:].bitcast(FP8X4),
             scales=m1_scales[:],
-            in_=m1_grouped[:].rearrange("p j r t -> p (j r t)"),
+            in_=m1_grouped[:].rearrange("p v r e t -> p (v r e t)"),
         )
 
         m_inv = inverse_norm(m_sum_sq, N_BLOCKS, 1.0, "m_inv")
+        quantise_k(0)
         m_inv_all = keep.tile([P, N], F32, name="m_inv_all")
         for h in range(HALVES):
-            spread = dots_psum.tile([P, BANK], F32, name="spread", tag="dots")
+            spread = banks.tile([P, BANK], F32, name="spread", tag="bank")
             for a in range(BANK // P):
                 j = h * (BANK // P) + a
                 nc.tensor.matmul(
@@ -138,7 +154,10 @@ def tile_memory_t_kernel(tc, key, memory, out):
                     start=True,
                     stop=True,
                 )
-            nc.vector.tensor_copy(out=m_inv_all[:, h * BANK : (h + 1) * BANK], in_=spread[:])
+            nc.vector.tensor_copy(
+                out=m_inv_all[:, h * BANK : (h + 1) * BANK].rearrange("p (u r e) -> p u r e", u=2, e=2),
+                in_=spread[:].rearrange("p (u e r) -> p u r e", u=2, e=2),
+            )
 
         m2_grouped = keep.tile([P, N_PASSES, D, PACK], BF16, name="m2_grouped", align_bytes=64)
         for c in range(N_PASSES):
@@ -153,27 +172,9 @@ def tile_memory_t_kernel(tc, key, memory, out):
         m2_codes = keep.tile([P, N_PASSES * D], U32, name="m2_codes", align_bytes=64)
         m2_scales = keep.tile([P, N_PASSES * D], U8, name="m2_scales", align_bytes=64)
 
-        k_sum_sq = {}
-        k_scale = {}
-        k_codes = {}
-        k_scales = {}
-
-        def quantise_k(g):
-            k_grouped = k_pool.tile([P, GROUP, P, PACK], BF16, name="k_grouped", bufs=1, align_bytes=64)
-            for j in range(0, GROUP, 2):
-                turn_words(k_sb[g][:], k_grouped[:], j, 2)
-            k_codes[g] = k_pool.tile([P, GROUP * P], U32, name="k_codes", align_bytes=64)
-            k_scales[g] = k_pool.tile([P, GROUP * P], U8, name="k_scales", align_bytes=64)
-            nc.vector.quantize_mx(
-                out=k_codes[g][:].bitcast(FP8X4),
-                scales=k_scales[g][:],
-                in_=k_grouped[:].rearrange("p j r t -> p (j r t)"),
-            )
-
         k_sum_sq[0] = stat.tile([P, GROUP], F32, name="k_sum_sq")
         for j in range(GROUP):
             sum_squares(k_sb[0], k_sum_sq[0], j)
-        quantise_k(0)
         k_scale[0] = inverse_norm(k_sum_sq[0], GROUP, PI_2, "k_inv")
 
         dots = {}
@@ -183,16 +184,14 @@ def tile_memory_t_kernel(tc, key, memory, out):
         sums = {}
         inv_sums = {}
         w_tiles = {}
-        w_turned = {}
         w_grouped = {}
         w_codes = {}
         w_scales = {}
-        out_acc = {}
 
         def first_matmul(i):
             g, j = divmod(i, GROUP)
             for h in range(HALVES):
-                dots[i, h] = dots_psum.tile([P, BANK], F32, name="dots", tag="dots")
+                dots[i, h] = banks.tile([P, BANK], F32, name="dots", tag="bank")
                 nc.tensor.matmul_mx(
                     out=dots[i, h][:],
                     lhsT=k_codes[g][:, j * P : (j + 1) * P].bitcast(FP8X4),
@@ -203,8 +202,7 @@ def tile_memory_t_kernel(tc, key, memory, out):
                     stop=True,
                 )
 
-        def sine(i):
-            g, j = divmod(i, GROUP)
+        def scaled_dots(i):
             a_tiles[i] = a_pool.tile([P, N], F32, name="a_tile")
             for h in range(HALVES):
                 nc.vector.tensor_tensor(
@@ -213,6 +211,11 @@ def tile_memory_t_kernel(tc, key, memory, out):
                     in1=m_inv_all[:, h * BANK : (h + 1) * BANK],
                     op=ALU.mult,
                 )
+            if (i + DOTS_TILES) // GROUP == i // GROUP:
+                first_matmul(i + DOTS_TILES)
+
+        def sine(i):
+            g, j = divmod(i, GROUP)
             nc.scalar.activation(
                 out=a_tiles[i][:], in_=a_tiles[i][:], func=ACT.Sin, scale=k_scale[g][:, j : j + 1]
             )
@@ -243,9 +246,9 @@ def tile_memory_t_kernel(tc, key, memory, out):
                 accum_out=sums[g][:, j : j + 1],
             )
             nc.vector.reciprocal(out=inv_sums[g][:, j : j + 1], in_=sums[g][:, j : j + 1])
-            w_tiles[i] = w_pool.tile([P, N], BF16, name="w_tile")
+            w_tiles[i] = w_pool.tile([P, N_PASSES, K_PASS], BF16, name="w_tile")
             nc.gpsimd.tensor_scalar(
-                out=w_tiles[i][:],
+                out=w_tiles[i][:].rearrange("p c f -> p (c f)"),
                 in0=a_tiles[i][:],
                 scalar1=inv_sums[g][:, j : j + 1],
                 scalar2=0.0,
@@ -254,30 +257,24 @@ def tile_memory_t_kernel(tc, key, memory, out):
             )
 
         def turn_w(i):
-            w_turned[i] = turn_psum.tile([P, N_BLOCKS, P], BF16, name="w_turned", tag="turn")
-            for f in range(N_BLOCKS):
-                nc.tensor.transpose(
-                    out=w_turned[i][:, f, :], in_=w_tiles[i][:, f * P : (f + 1) * P], identity=ident_bf16[:]
-                )
+            turned = turn_words(w_tiles[i][:])
+            w_grouped[i] = short.tile([P, N_PASSES, P, PACK], BF16, name="w_grouped", align_bytes=64)
+            nc.vector.tensor_copy(out=w_grouped[i][:].bitcast(F32), in_=turned[:].rearrange("p c u r -> p c r u"))
 
-        def group_w(i):
-            w_grouped[i] = post.tile([P, N_PASSES, P, PACK], BF16, name="w_grouped", align_bytes=64)
-            nc.vector.tensor_copy(
-                out=w_grouped[i][:], in_=w_turned[i][:].rearrange("p (c t) r -> p c r t", c=N_PASSES)
-            )
-
-        def second_matmul(i):
-            w_codes[i] = post.tile([P, N_PASSES * P], U32, name="w_codes", align_bytes=64)
-            w_scales[i] = post.tile([P, N_PASSES * P], U8, name="w_scales", align_bytes=64)
+        def quantise_w(i):
+            w_codes[i] = w_pool.tile([P, N_PASSES * P], U32, name="w_codes", align_bytes=64)
+            w_scales[i] = w_pool.tile([P, N_PASSES * P], U8, name="w_scales", align_bytes=64)
             nc.vector.quantize_mx(
                 out=w_codes[i][:].bitcast(FP8X4),
                 scales=w_scales[i][:],
                 in_=w_grouped[i][:].rearrange("p c r t -> p (c r t)"),
             )
-            out_acc[i] = out_psum.tile([P, D], F32, name="out_acc")
+
+        def second_matmul_and_store(i):
+            out_acc = out_psum.tile([P, D], F32, name="out_acc")
             for c in range(N_PASSES):
                 nc.tensor.matmul_mx(
-                    out=out_acc[i][:],
+                    out=out_acc[:],
                     lhsT=w_codes[i][:, c * P : (c + 1) * P].bitcast(FP8X4),
                     lhsT_scale=w_scales[i][:, c * P : (c + 1) * P],
                     rhs=m2_codes[:, c * D : (c + 1) * D].bitcast(FP8X4),
@@ -285,39 +282,26 @@ def tile_memory_t_kernel(tc, key, memory, out):
                     start=(c == 0),
                     stop=(c == N_PASSES - 1),
                 )
-
-        def store(i):
-            out_sb = post.tile([P, D], F32, name="out_sb")
-            nc.scalar.copy(out=out_sb[:], in_=out_acc[i][:])
+            out_sb = short.tile([P, D], F32, name="out_sb", bufs=GROUP)
+            nc.scalar.copy(out=out_sb[:], in_=out_acc[:])
             nc.sync.dma_start(out=out_rows[:, i, :], in_=out_sb[:])
 
-        def finish_step(s, lo, hi):
-            if lo <= s + 1 < hi:
-                turn_w(s + 1)
-            if lo <= s - 2 < hi:
-                store(s - 2)
-            if lo <= s < hi:
-                group_w(s)
-            if lo <= s - 1 < hi:
-                second_matmul(s - 1)
-
-        first_matmul(0)
+        for i in range(DOTS_TILES):
+            first_matmul(i)
         for g in range(GROUPS + 1):
             here = g * GROUP
-            lo, hi = here - GROUP, here
+            lo = here - GROUP
             if g + 2 < GROUPS:
                 load_k(g + 2)
+
+            if g < GROUPS:
+                for j in range(GROUP):
+                    scaled_dots(here + j)
+                for j in range(GROUP):
+                    sine(here + j)
             if g + 1 < GROUPS:
                 k_sum_sq[g + 1] = stat.tile([P, GROUP], F32, name="k_sum_sq")
-
-            for j in range(GROUP):
-                if g < GROUPS:
-                    if j + 1 < GROUP:
-                        first_matmul(here + j + 1)
-                    sine(here + j)
-                if g > 0:
-                    finish_step(lo + j, lo, hi)
-                if g + 1 < GROUPS:
+                for j in range(GROUP):
                     sum_squares(k_sb[g + 1], k_sum_sq[g + 1], j)
             if g == 0:
                 nc.vector.quantize_mx(
@@ -326,26 +310,32 @@ def tile_memory_t_kernel(tc, key, memory, out):
                     in_=m2_grouped[:].rearrange("p c d t -> p (c d t)"),
                 )
             else:
-                finish_step(hi, lo, hi)
-                finish_step(hi + 1, lo, hi)
-            if g == GROUPS:
-                break
+                for j in range(GROUP + 3):
+                    if j < GROUP:
+                        turn_w(lo + j)
+                    if 1 <= j <= GROUP:
+                        quantise_w(lo + j - 1)
+                    if g == GROUPS and j >= 3:
+                        second_matmul_and_store(lo + j - 3)
+            if g + 1 < GROUPS:
+                quantise_k(g + 1)
+                for i in range(DOTS_TILES):
+                    first_matmul(here + GROUP + i)
 
             if g + 1 < GROUPS:
                 k_scale[g + 1] = inverse_norm(k_sum_sq[g + 1], GROUP, PI_2, "k_inv")
-            for j in range(GROUP):
-                inverse_cosine(here + j)
+            if g < GROUPS:
+                for j in range(GROUP):
+                    inverse_cosine(here + j)
+                neg_max[g] = stat.tile([P, GROUP], F32, name="neg_max")
+                sums[g] = stat.tile([P, GROUP], F32, name="sums")
+                inv_sums[g] = stat.tile([P, GROUP], F32, name="inv_sums")
 
-            neg_max[g] = stat.tile([P, GROUP], F32, name="neg_max")
-            sums[g] = stat.tile([P, GROUP], F32, name="sums")
-            inv_sums[g] = stat.tile([P, GROUP], F32, name="inv_sums")
             for j in range(GROUP + EXP_LAG):
-                if j < GROUP:
+                if g < GROUPS and j < GROUP:
                     tangent_and_max(here + j)
                 if j >= EXP_LAG:
-                    softmax(here + j - EXP_LAG)
-
-            if g + 1 < GROUPS:
-                quantise_k(g + 1)
-                first_matmul(here + GROUP)
-            turn_w(here)
+                    if g < GROUPS:
+                        softmax(here + j - EXP_LAG)
+                    if 0 < g < GROUPS:
+                        second_matmul_and_store(lo + j - EXP_LAG)

@@ -24,6 +24,7 @@ N_PASSES = N // K_PASS
 BANK = 512
 HALVES = N // BANK
 DOTS_TILES = 2
+SCALAR_SQUARES = 2
 EXP_LAG = 4
 PI_2 = 3.14159 / 2
 EPS = 1e-8
@@ -46,23 +47,23 @@ def tile_memory_t_kernel(tc, key, memory, out):
         a_pool = stack.enter_context(tc.tile_pool(name="a_pool", bufs=GROUP + 4))
         b_pool = stack.enter_context(tc.tile_pool(name="b_pool", bufs=GROUP))
         w_pool = stack.enter_context(tc.tile_pool(name="w_pool", bufs=GROUP + 1))
-        short = stack.enter_context(tc.tile_pool(name="short", bufs=3))
+        short = stack.enter_context(tc.tile_pool(name="short", bufs=GROUP))
         banks = stack.enter_context(tc.psum_pool(name="banks", bufs=6))
         out_psum = stack.enter_context(tc.psum_pool(name="out_psum", bufs=2))
 
         def inverse_norm(sum_sq, width, factor, name):
             rough = stat.tile([P, width], F32, name=name + "_rough")
             nc.scalar.activation(out=rough[:], in_=sum_sq[:], func=ACT.Abs_reciprocal_sqrt)
-            nc.vector.tensor_scalar_min(out=rough[:], in0=rough[:], scalar1=1.0 / EPS)
+            nc.gpsimd.tensor_scalar_min(out=rough[:], in0=rough[:], scalar1=1.0 / EPS)
             step = stat.tile([P, width], F32, name=name + "_step")
-            nc.vector.tensor_tensor(out=step[:], in0=sum_sq[:], in1=rough[:], op=ALU.mult)
-            nc.vector.tensor_tensor(out=step[:], in0=step[:], in1=rough[:], op=ALU.mult)
-            nc.vector.tensor_scalar(
+            nc.gpsimd.tensor_tensor(out=step[:], in0=sum_sq[:], in1=rough[:], op=ALU.mult)
+            nc.gpsimd.tensor_tensor(out=step[:], in0=step[:], in1=rough[:], op=ALU.mult)
+            nc.gpsimd.tensor_scalar(
                 out=step[:], in0=step[:], scalar1=-0.5, scalar2=1.5, op0=ALU.mult, op1=ALU.add
             )
             fine = stat.tile([P, width], F32, name=name + "_fine")
-            nc.vector.tensor_tensor(out=fine[:], in0=rough[:], in1=step[:], op=ALU.mult)
-            nc.vector.tensor_scalar(
+            nc.gpsimd.tensor_tensor(out=fine[:], in0=rough[:], in1=step[:], op=ALU.mult)
+            nc.gpsimd.tensor_scalar(
                 out=fine[:], in0=fine[:], scalar1=1.0 / EPS, scalar2=factor, op0=ALU.min, op1=ALU.mult
             )
             return fine
@@ -107,19 +108,23 @@ def tile_memory_t_kernel(tc, key, memory, out):
         k_codes = {}
         k_scales = {}
 
-        def quantise_k(g):
-            k_grouped = k_pool.tile([P, GROUP, P, PACK], BF16, name="k_grouped", bufs=1, align_bytes=64)
+        k_grouped = {}
+
+        def turn_k(g):
+            k_grouped[g] = k_pool.tile([P, GROUP, P, PACK], BF16, name="k_grouped", bufs=1, align_bytes=64)
             for j in range(0, GROUP, 2):
                 turned = turn_words(k_sb[g][:, j : j + 2, :])
                 nc.vector.tensor_copy(
-                    out=k_grouped[:, j : j + 2, :, :].bitcast(F32), in_=turned[:].rearrange("p a u r -> p a r u")
+                    out=k_grouped[g][:, j : j + 2, :, :].bitcast(F32), in_=turned[:].rearrange("p a u r -> p a r u")
                 )
+
+        def quantise_k(g):
             k_codes[g] = k_pool.tile([P, GROUP * P], U32, name="k_codes", align_bytes=64)
             k_scales[g] = k_pool.tile([P, GROUP * P], U8, name="k_scales", align_bytes=64)
             nc.vector.quantize_mx(
                 out=k_codes[g][:].bitcast(FP8X4),
                 scales=k_scales[g][:],
-                in_=k_grouped[:].rearrange("p j r t -> p (j r t)"),
+                in_=k_grouped[g][:].rearrange("p j r t -> p (j r t)"),
             )
 
         m_sum_sq = keep.tile([P, N_BLOCKS], F32, name="m_sum_sq")
@@ -141,6 +146,7 @@ def tile_memory_t_kernel(tc, key, memory, out):
         )
 
         m_inv = inverse_norm(m_sum_sq, N_BLOCKS, 1.0, "m_inv")
+        turn_k(0)
         quantise_k(0)
         m_inv_all = keep.tile([P, N], F32, name="m_inv_all")
         for h in range(HALVES):
@@ -160,15 +166,6 @@ def tile_memory_t_kernel(tc, key, memory, out):
             )
 
         m2_grouped = keep.tile([P, N_PASSES, D, PACK], BF16, name="m2_grouped", align_bytes=64)
-        for c in range(N_PASSES):
-            nc.gpsimd.tensor_scalar(
-                out=m2_grouped[:, c, :, :],
-                in0=m_sb[:, c * PACK : (c + 1) * PACK, :].rearrange("p t d -> p d t"),
-                scalar1=1.0,
-                scalar2=0.0,
-                op0=ALU.mult,
-                op1=ALU.add,
-            )
         m2_codes = keep.tile([P, N_PASSES * D], U32, name="m2_codes", align_bytes=64)
         m2_scales = keep.tile([P, N_PASSES * D], U8, name="m2_scales", align_bytes=64)
 
@@ -219,19 +216,26 @@ def tile_memory_t_kernel(tc, key, memory, out):
             nc.scalar.activation(
                 out=a_tiles[i][:], in_=a_tiles[i][:], func=ACT.Sin, scale=k_scale[g][:, j : j + 1]
             )
+
+        def square(i):
             b_tiles[i] = b_pool.tile([P, N], F32, name="b_tile")
-            nc.gpsimd.tensor_tensor(out=b_tiles[i][:], in0=a_tiles[i][:], in1=a_tiles[i][:], op=ALU.mult)
+            if i % GROUP < GROUP - SCALAR_SQUARES:
+                nc.gpsimd.tensor_tensor(out=b_tiles[i][:], in0=a_tiles[i][:], in1=a_tiles[i][:], op=ALU.mult)
+            else:
+                nc.scalar.activation(out=b_tiles[i][:], in_=a_tiles[i][:], func=ACT.Square)
 
         def inverse_cosine(i):
             nc.scalar.activation(
                 out=b_tiles[i][:], in_=b_tiles[i][:], func=ACT.Abs_reciprocal_sqrt, scale=-1.0, bias=1.0
             )
 
-        def tangent_and_max(i):
-            g, j = divmod(i, GROUP)
+        def tangent(i):
             nc.vector.scalar_tensor_tensor(
                 out=a_tiles[i][:], in0=b_tiles[i][:], scalar=HUGE, in1=a_tiles[i][:], op0=ALU.min, op1=ALU.mult
             )
+
+        def row_max(i):
+            g, j = divmod(i, GROUP)
             nc.vector.tensor_reduce(
                 out=neg_max[g][:, j : j + 1], in_=a_tiles[i][:], axis=AXIS.X, op=ALU.max, negate=True
             )
@@ -282,7 +286,7 @@ def tile_memory_t_kernel(tc, key, memory, out):
                     start=(c == 0),
                     stop=(c == N_PASSES - 1),
                 )
-            out_sb = short.tile([P, D], F32, name="out_sb", bufs=GROUP)
+            out_sb = short.tile([P, D], F32, name="out_sb")
             nc.scalar.copy(out=out_sb[:], in_=out_acc[:])
             nc.sync.dma_start(out=out_rows[:, i, :], in_=out_sb[:])
 
@@ -299,28 +303,43 @@ def tile_memory_t_kernel(tc, key, memory, out):
                     scaled_dots(here + j)
                 for j in range(GROUP):
                     sine(here + j)
+                for j in range(GROUP):
+                    square(here + j)
             if g + 1 < GROUPS:
                 k_sum_sq[g + 1] = stat.tile([P, GROUP], F32, name="k_sum_sq")
                 for j in range(GROUP):
                     sum_squares(k_sb[g + 1], k_sum_sq[g + 1], j)
+            if 0 < g < GROUPS:
+                for j in range(GROUP):
+                    turn_w(lo + j)
+            if g + 1 < GROUPS:
+                turn_k(g + 1)
             if g == 0:
+                for c in range(N_PASSES):
+                    nc.vector.tensor_copy(
+                        out=m2_grouped[:, c, :, :],
+                        in_=m_sb[:, c * PACK : (c + 1) * PACK, :].rearrange("p t d -> p d t"),
+                    )
                 nc.vector.quantize_mx(
                     out=m2_codes[:].bitcast(FP8X4),
                     scales=m2_scales[:],
                     in_=m2_grouped[:].rearrange("p c d t -> p (c d t)"),
                 )
-            else:
+            if 0 < g < GROUPS:
+                for j in range(GROUP):
+                    quantise_w(lo + j)
+            if g + 1 < GROUPS:
+                quantise_k(g + 1)
+                for i in range(DOTS_TILES):
+                    first_matmul(here + GROUP + i)
+            if g == GROUPS:
                 for j in range(GROUP + 3):
                     if j < GROUP:
                         turn_w(lo + j)
                     if 1 <= j <= GROUP:
                         quantise_w(lo + j - 1)
-                    if g == GROUPS and j >= 3:
+                    if j >= 3:
                         second_matmul_and_store(lo + j - 3)
-            if g + 1 < GROUPS:
-                quantise_k(g + 1)
-                for i in range(DOTS_TILES):
-                    first_matmul(here + GROUP + i)
 
             if g + 1 < GROUPS:
                 k_scale[g + 1] = inverse_norm(k_sum_sq[g + 1], GROUP, PI_2, "k_inv")
@@ -333,7 +352,9 @@ def tile_memory_t_kernel(tc, key, memory, out):
 
             for j in range(GROUP + EXP_LAG):
                 if g < GROUPS and j < GROUP:
-                    tangent_and_max(here + j)
+                    tangent(here + j)
+                if g < GROUPS and 1 <= j <= GROUP:
+                    row_max(here + j - 1)
                 if j >= EXP_LAG:
                     if g < GROUPS:
                         softmax(here + j - EXP_LAG)

@@ -17,15 +17,20 @@ PACK = 4
 K_PASS = P * PACK
 B, N, D = 4096, 1024, 512
 TILES = B // P
-GROUP = 8
-GROUPS = TILES // GROUP
+PAIRS = TILES // 2
+GROUP_SIZES = (8, 8, 8, 8)
 N_BLOCKS = N // P
 N_PASSES = N // K_PASS
 BANK = 512
 HALVES = N // BANK
-DOTS_TILES = 2
-SCALAR_SQUARES = 2
-EXP_LAG = 4
+DOTS_BANKS = 3
+TURN_BANKS = 3
+OUT_BANKS = 2
+SCALED_AHEAD = 3
+TAN_AHEAD = 4
+LAGS = (2, 2, 3, 4, 5)
+SQUARES = ["GGGGGSGS","GGGGGSGS","GGGGGSGS","GGGGGSGS"]
+VECTOR_NORMS = 3
 PI_2 = 3.14159 / 2
 EPS = 1e-8
 HUGE = 3.0e38
@@ -42,138 +47,244 @@ def tile_memory_t_kernel(tc, key, memory, out):
     with ExitStack() as stack:
         stack.enter_context(tc.manual_schedule())
         keep = stack.enter_context(tc.tile_pool(name="keep", bufs=1))
-        k_pool = stack.enter_context(tc.tile_pool(name="k_pool", bufs=2))
-        stat = stack.enter_context(tc.tile_pool(name="stat", bufs=2))
-        a_pool = stack.enter_context(tc.tile_pool(name="a_pool", bufs=GROUP + 4))
-        b_pool = stack.enter_context(tc.tile_pool(name="b_pool", bufs=GROUP))
-        w_pool = stack.enter_context(tc.tile_pool(name="w_pool", bufs=GROUP + 1))
-        short = stack.enter_context(tc.tile_pool(name="short", bufs=GROUP))
-        banks = stack.enter_context(tc.psum_pool(name="banks", bufs=6))
-        out_psum = stack.enter_context(tc.psum_pool(name="out_psum", bufs=2))
+        k_in = stack.enter_context(tc.tile_pool(name="k_in", bufs=6))
+        k_out = stack.enter_context(tc.tile_pool(name="k_out", bufs=2))
+        grouped_pool = stack.enter_context(tc.tile_pool(name="grouped_pool", bufs=7))
+        w_out = stack.enter_context(tc.tile_pool(name="w_out", bufs=1))
+        stat = stack.enter_context(tc.tile_pool(name="stat", bufs=1))
+        a_pool = stack.enter_context(tc.tile_pool(name="a_pool", bufs=max(GROUP_SIZES) + SCALED_AHEAD))
+        b_pool = stack.enter_context(tc.tile_pool(name="b_pool", bufs=max(GROUP_SIZES)))
+        w_pool = stack.enter_context(tc.tile_pool(name="w_pool", bufs=9))
+        out_pool = stack.enter_context(tc.tile_pool(name="out_pool", bufs=3))
+        dots_psum = stack.enter_context(tc.psum_pool(name="dots_psum", bufs=DOTS_BANKS))
+        turn_psum = stack.enter_context(tc.psum_pool(name="turn_psum", bufs=TURN_BANKS))
+        out_psum = stack.enter_context(tc.psum_pool(name="out_psum", bufs=OUT_BANKS))
 
-        def inverse_norm(sum_sq, width, factor, name):
+        def rough_inverse(sum_sq, width, name):
             rough = stat.tile([P, width], F32, name=name + "_rough")
             nc.scalar.activation(out=rough[:], in_=sum_sq[:], func=ACT.Abs_reciprocal_sqrt)
-            nc.gpsimd.tensor_scalar_min(out=rough[:], in0=rough[:], scalar1=1.0 / EPS)
+            return rough
+
+        def newton(engine, sum_sq, rough, width, factor, name):
+            engine.tensor_scalar_min(out=rough[:], in0=rough[:], scalar1=1.0 / EPS)
             step = stat.tile([P, width], F32, name=name + "_step")
-            nc.gpsimd.tensor_tensor(out=step[:], in0=sum_sq[:], in1=rough[:], op=ALU.mult)
-            nc.gpsimd.tensor_tensor(out=step[:], in0=step[:], in1=rough[:], op=ALU.mult)
-            nc.gpsimd.tensor_scalar(
+            engine.tensor_tensor(out=step[:], in0=sum_sq[:], in1=rough[:], op=ALU.mult)
+            engine.tensor_tensor(out=step[:], in0=step[:], in1=rough[:], op=ALU.mult)
+            engine.tensor_scalar(
                 out=step[:], in0=step[:], scalar1=-0.5, scalar2=1.5, op0=ALU.mult, op1=ALU.add
             )
             fine = stat.tile([P, width], F32, name=name + "_fine")
-            nc.gpsimd.tensor_tensor(out=fine[:], in0=rough[:], in1=step[:], op=ALU.mult)
-            nc.gpsimd.tensor_scalar(
+            engine.tensor_tensor(out=fine[:], in0=rough[:], in1=step[:], op=ALU.mult)
+            engine.tensor_scalar(
                 out=fine[:], in0=fine[:], scalar1=1.0 / EPS, scalar2=factor, op0=ALU.min, op1=ALU.mult
             )
             return fine
 
-        def turn_words(rows):
+        turned = {}
+
+        def turn(name, rows):
             words = rows.bitcast(F32)
-            turned = banks.tile([P, 2, 2, P], F32, name="turned", tag="bank")
+            turned[name] = turn_psum.tile([P, 2, 2, P], F32, name="turned", tag="turned")
             for a in range(2):
                 for u in range(2):
                     nc.tensor.transpose(
-                        out=turned[:, a, u, :], in_=words[:, a, u * P : (u + 1) * P], identity=ident_f32[:]
+                        out=turned[name][:, a, u, :], in_=words[:, a, u * P : (u + 1) * P], identity=ident_f32[:]
                     )
-            return turned
+
+        def grouped_tile(shape):
+            return grouped_pool.tile(shape, BF16, name="grouped", tag="grouped", align_bytes=64)
 
         one = keep.tile([P, 1], F32, name="one")
         nc.vector.memset(one[:], 1.0)
         nc.scalar.activation(out=one[:], in_=one[:], func=ACT.Abs_reciprocal_sqrt)
 
         m_sb = keep.tile([P, N_BLOCKS, D], BF16, name="m_sb")
-        nc.sync.dma_start(out=m_sb[:].rearrange("p (c t) d -> p c t d", c=N_PASSES), in_=mem_rows)
+        for c in range(N_PASSES):
+            nc.sync.dma_start(out=m_sb[:, c * PACK : (c + 1) * PACK, :], in_=mem_rows[:, c, :, :])
+
         k_sb = {}
+        loads = list(range(PAIRS))
 
-        def load_k(g):
-            k_sb[g] = k_pool.tile([P, GROUP, D], BF16, name="k_sb")
-            nc.sync.dma_start(out=k_sb[g][:], in_=key_rows[:, g * GROUP : (g + 1) * GROUP, :])
+        def load_k():
+            if loads:
+                q = loads[0]
+                k_sb[q] = k_in.tile([P, 2, D], BF16, name="k_sb")
+                nc.sync.dma_start(out=k_sb[q][:], in_=key_rows[:, 2 * q : 2 * q + 2, :])
+                loads.remove(q)
 
-        load_k(0)
-        load_k(1)
+        for q in range(6):
+            load_k()
 
         ident_f32 = keep.tile([P, P], F32, name="ident_f32")
         make_identity(nc, ident_f32[:])
 
-        squares = keep.tile([P, GROUP, D], BF16, name="squares")
+        groups = len(GROUP_SIZES)
+        group_of = {}
+        first_of = []
+        for g, size in enumerate(GROUP_SIZES):
+            first_of.append(len(group_of))
+            for j in range(size):
+                group_of[first_of[g] + j] = (g, j)
 
-        def sum_squares(rows_sb, sum_sq, j):
-            nc.scalar.activation(
-                out=squares[:, j, :], in_=rows_sb[:, j, :], func=ACT.Square, accum_out=sum_sq[:, j : j + 1]
-            )
+        def chunks(size, largest):
+            runs = []
+            j = 0
+            while j < size:
+                count = largest
+                while j + count > size:
+                    count //= 2
+                runs.append((j, count))
+                j += count
+            return runs
 
-        k_sum_sq = {}
-        k_scale = {}
+        k_chunk = {}
         k_codes = {}
         k_scales = {}
+        k_sum_sq = {}
+        k_scale = {}
+        coded = []
+        diag = keep.tile([P, P], BF16, name="diag")
 
-        k_grouped = {}
+        def k_place(i):
+            g, j = group_of[i]
+            for first, count in chunks(GROUP_SIZES[g], 8):
+                if first <= j < first + count:
+                    if (g, first) not in k_chunk:
+                        k_chunk[g, first] = grouped_tile([P, 8, P, PACK])
+                    return k_chunk[g, first], j - first
 
-        def turn_k(g):
-            k_grouped[g] = k_pool.tile([P, GROUP, P, PACK], BF16, name="k_grouped", bufs=1, align_bytes=64)
-            for j in range(0, GROUP, 2):
-                turned = turn_words(k_sb[g][:, j : j + 2, :])
-                nc.vector.tensor_copy(
-                    out=k_grouped[g][:, j : j + 2, :, :].bitcast(F32), in_=turned[:].rearrange("p a u r -> p a r u")
-                )
+        def turn_k(q):
+            turn(("k", q), k_sb[q][:])
+            load_k()
+
+        def group_k(q, engine=None):
+            rows, j = k_place(2 * q)
+            (engine or nc.vector.tensor_copy)(
+                out=rows[:, j : j + 2, :, :].bitcast(F32),
+                in_=turned["k", q][:].rearrange("p a u r -> p a r u"),
+            )
 
         def quantise_k(g):
-            k_codes[g] = k_pool.tile([P, GROUP * P], U32, name="k_codes", align_bytes=64)
-            k_scales[g] = k_pool.tile([P, GROUP * P], U8, name="k_scales", align_bytes=64)
-            nc.vector.quantize_mx(
-                out=k_codes[g][:].bitcast(FP8X4),
-                scales=k_scales[g][:],
-                in_=k_grouped[g][:].rearrange("p j r t -> p (j r t)"),
-            )
+            size = GROUP_SIZES[g]
+            k_codes[g] = k_out.tile([P, max(GROUP_SIZES) * P], U32, name="k_codes", align_bytes=64)
+            k_scales[g] = k_out.tile([P, max(GROUP_SIZES) * P], U8, name="k_scales", align_bytes=64)
+            for j, count in chunks(size, 8):
+                rows, at = k_place(first_of[g] + j)
+                nc.vector.quantize_mx(
+                    out=k_codes[g][:, j * P : (j + count) * P].bitcast(FP8X4),
+                    scales=k_scales[g][:, j * P : (j + count) * P],
+                    in_=rows[:, 0:count, :, :].rearrange("p a r t -> p (a r t)"),
+                )
+                for n in range(j, j + count):
+                    coded.append(first_of[g] + n)
 
+        gram = {}
+
+        def gram_k(q):
+            gram[q] = turn_psum.tile([P, 2, P], F32, name="gram", tag="turned")
+            rows, j = k_place(2 * q)
+            for a in range(2):
+                for t in range(PACK):
+                    nc.tensor.matmul(
+                        out=gram[q][:, a, :],
+                        lhsT=rows[:, j + a, :, t],
+                        rhs=rows[:, j + a, :, t],
+                        start=(t == 0),
+                        stop=(t == PACK - 1),
+                    )
+
+        def sum_squares_k(q):
+            for a in range(2):
+                g, j = group_of[2 * q + a]
+                if j == 0:
+                    k_sum_sq[g] = stat.tile([P, GROUP_SIZES[g]], F32, name="k_sum_sq%d" % g)
+                nc.vector.scalar_tensor_tensor(
+                    out=diag[:],
+                    in0=gram[q][:, a, :],
+                    scalar=1.0,
+                    in1=ident_f32[:],
+                    op0=ALU.mult,
+                    op1=ALU.mult,
+                    accum_out=k_sum_sq[g][:, j : j + 1],
+                )
+
+        squares = keep.tile([P, 2, D], BF16, name="squares")
         m_sum_sq = keep.tile([P, N_BLOCKS], F32, name="m_sum_sq")
-        for j in range(N_BLOCKS):
-            sum_squares(m_sb, m_sum_sq, j)
-
-        m1_grouped = keep.tile([P, N_BLOCKS // 2, P, 2, PACK], BF16, name="m1_grouped", align_bytes=64)
-        for v in range(N_BLOCKS // 2):
-            turned = turn_words(m_sb[:, 2 * v : 2 * v + 2, :])
-            nc.vector.tensor_copy(
-                out=m1_grouped[:, v, :, :, :].bitcast(F32), in_=turned[:].rearrange("p e u r -> p r e u")
+        for j in range(VECTOR_NORMS, N_BLOCKS):
+            nc.scalar.activation(
+                out=squares[:, 0, :], in_=m_sb[:, j, :], func=ACT.Square, accum_out=m_sum_sq[:, j : j + 1]
             )
+        for j in range(VECTOR_NORMS):
+            nc.vector.scalar_tensor_tensor(
+                out=squares[:, 1, :],
+                in0=m_sb[:, j, :],
+                scalar=1.0,
+                in1=m_sb[:, j, :],
+                op0=ALU.mult,
+                op1=ALU.mult,
+                accum_out=m_sum_sq[:, j : j + 1],
+            )
+        m_rough = rough_inverse(m_sum_sq, N_BLOCKS, "m_inv")
+        m1_grouped = [grouped_tile([P, 2, P, 2, PACK]) for h in range(HALVES)]
         m1_codes = keep.tile([P, N], U32, name="m1_codes", align_bytes=64)
         m1_scales = keep.tile([P, N], U8, name="m1_scales", align_bytes=64)
-        nc.vector.quantize_mx(
-            out=m1_codes[:].bitcast(FP8X4),
-            scales=m1_scales[:],
-            in_=m1_grouped[:].rearrange("p v r e t -> p (v r e t)"),
-        )
-
-        m_inv = inverse_norm(m_sum_sq, N_BLOCKS, 1.0, "m_inv")
-        turn_k(0)
-        quantise_k(0)
-        m_inv_all = keep.tile([P, N], F32, name="m_inv_all")
-        for h in range(HALVES):
-            spread = banks.tile([P, BANK], F32, name="spread", tag="bank")
-            for a in range(BANK // P):
-                j = h * (BANK // P) + a
-                nc.tensor.matmul(
-                    out=spread[:, a * P : (a + 1) * P],
-                    lhsT=m_inv[:, j : j + 1].to_broadcast([P, P]),
-                    rhs=ident_f32[:],
-                    start=True,
-                    stop=True,
-                )
+        for v in range(N_BLOCKS // 2):
+            turn(("m", v), m_sb[:, 2 * v : 2 * v + 2, :])
+            h, half = divmod(v, 2)
             nc.vector.tensor_copy(
+                out=m1_grouped[h][:, half, :, :, :].bitcast(F32),
+                in_=turned["m", v][:].rearrange("p e u r -> p r e u"),
+            )
+        first_pairs = list(range(GROUP_SIZES[0] // 2))
+        m_inv = newton(nc.vector, m_sum_sq, m_rough, N_BLOCKS, 1.0, "m_inv")
+        for q in first_pairs:
+            turn_k(q)
+            group_k(q, nc.scalar.copy if q < 2 else None)
+            if q == 1:
+                m_inv_all = keep.tile([P, N], F32, name="m_inv_all")
+                spreads = []
+                for h in range(HALVES):
+                    spread = dots_psum.tile([P, BANK], F32, name="spread", tag="dots")
+                    for a in range(BANK // P):
+                        j = h * (BANK // P) + a
+                        nc.tensor.matmul(
+                            out=spread[:, a * P : (a + 1) * P],
+                            lhsT=m_inv[:, j : j + 1].to_broadcast([P, P]),
+                            rhs=ident_f32[:],
+                            start=True,
+                            stop=True,
+                        )
+                    spreads.append(spread)
+        for h in range(HALVES):
+            nc.vector.quantize_mx(
+                out=m1_codes[:, h * BANK : (h + 1) * BANK].bitcast(FP8X4),
+                scales=m1_scales[:, h * BANK : (h + 1) * BANK],
+                in_=m1_grouped[h][:].rearrange("p v r e t -> p (v r e t)"),
+            )
+        k_sum_sq[0] = stat.tile([P, GROUP_SIZES[0]], F32, name="k_sum_sq0")
+        for j in range(GROUP_SIZES[0]):
+            nc.scalar.activation(
+                out=squares[:, 0, :], in_=k_sb[j // 2][:, j % 2, :], func=ACT.Square, accum_out=k_sum_sq[0][:, j : j + 1]
+            )
+        for h in range(HALVES):
+            (nc.vector.tensor_copy, nc.vector.tensor_copy)[h](
                 out=m_inv_all[:, h * BANK : (h + 1) * BANK].rearrange("p (u r e) -> p u r e", u=2, e=2),
-                in_=spread[:].rearrange("p (u e r) -> p u r e", u=2, e=2),
+                in_=spreads[h][:].rearrange("p (u e r) -> p u r e", u=2, e=2),
             )
 
-        m2_grouped = keep.tile([P, N_PASSES, D, PACK], BF16, name="m2_grouped", align_bytes=64)
+        m2_grouped = grouped_tile([P, N_PASSES, D, PACK])
         m2_codes = keep.tile([P, N_PASSES * D], U32, name="m2_codes", align_bytes=64)
         m2_scales = keep.tile([P, N_PASSES * D], U8, name="m2_scales", align_bytes=64)
-
-        k_sum_sq[0] = stat.tile([P, GROUP], F32, name="k_sum_sq")
-        for j in range(GROUP):
-            sum_squares(k_sb[0], k_sum_sq[0], j)
-        k_scale[0] = inverse_norm(k_sum_sq[0], GROUP, PI_2, "k_inv")
-
+        for c in range(N_PASSES):
+            for d in range(0, D, P):
+                nc.gpsimd.tensor_scalar(
+                    out=m2_grouped[:, c, d : d + P, :],
+                    in0=m_sb[:, c * PACK : (c + 1) * PACK, d : d + P].rearrange("p t d -> p d t"),
+                    scalar1=1.0,
+                    scalar2=0.0,
+                    op0=ALU.mult,
+                    op1=ALU.add,
+                )
         dots = {}
         a_tiles = {}
         b_tiles = {}
@@ -184,11 +295,17 @@ def tile_memory_t_kernel(tc, key, memory, out):
         w_grouped = {}
         w_codes = {}
         w_scales = {}
+        out_acc = {}
+        dots_order = [(i, h) for i in range(TILES) for h in range(HALVES)]
+        scaled_order = list(dots_order)
 
-        def first_matmul(i):
-            g, j = divmod(i, GROUP)
-            for h in range(HALVES):
-                dots[i, h] = banks.tile([P, BANK], F32, name="dots", tag="bank")
+        def first_matmuls():
+            while dots_order and len(dots_order) > len(scaled_order) - DOTS_BANKS:
+                i, h = dots_order[0]
+                g, j = group_of[i]
+                if i not in coded:
+                    return
+                dots[i, h] = dots_psum.tile([P, BANK], F32, name="dots", tag="dots")
                 nc.tensor.matmul_mx(
                     out=dots[i, h][:],
                     lhsT=k_codes[g][:, j * P : (j + 1) * P].bitcast(FP8X4),
@@ -198,6 +315,7 @@ def tile_memory_t_kernel(tc, key, memory, out):
                     start=True,
                     stop=True,
                 )
+                dots_order.remove((i, h))
 
         def scaled_dots(i):
             a_tiles[i] = a_pool.tile([P, N], F32, name="a_tile")
@@ -208,21 +326,22 @@ def tile_memory_t_kernel(tc, key, memory, out):
                     in1=m_inv_all[:, h * BANK : (h + 1) * BANK],
                     op=ALU.mult,
                 )
-            if (i + DOTS_TILES) // GROUP == i // GROUP:
-                first_matmul(i + DOTS_TILES)
+                scaled_order.remove((i, h))
+                first_matmuls()
 
         def sine(i):
-            g, j = divmod(i, GROUP)
+            g, j = group_of[i]
             nc.scalar.activation(
                 out=a_tiles[i][:], in_=a_tiles[i][:], func=ACT.Sin, scale=k_scale[g][:, j : j + 1]
             )
 
-        def square(i):
+        def square(i, engine):
             b_tiles[i] = b_pool.tile([P, N], F32, name="b_tile")
-            if i % GROUP < GROUP - SCALAR_SQUARES:
-                nc.gpsimd.tensor_tensor(out=b_tiles[i][:], in0=a_tiles[i][:], in1=a_tiles[i][:], op=ALU.mult)
-            else:
+            if engine == "S":
                 nc.scalar.activation(out=b_tiles[i][:], in_=a_tiles[i][:], func=ACT.Square)
+            else:
+                e = nc.gpsimd if engine == "G" else nc.vector
+                e.tensor_tensor(out=b_tiles[i][:], in0=a_tiles[i][:], in1=a_tiles[i][:], op=ALU.mult)
 
         def inverse_cosine(i):
             nc.scalar.activation(
@@ -235,13 +354,13 @@ def tile_memory_t_kernel(tc, key, memory, out):
             )
 
         def row_max(i):
-            g, j = divmod(i, GROUP)
+            g, j = group_of[i]
             nc.vector.tensor_reduce(
                 out=neg_max[g][:, j : j + 1], in_=a_tiles[i][:], axis=AXIS.X, op=ALU.max, negate=True
             )
 
-        def softmax(i):
-            g, j = divmod(i, GROUP)
+        def exponential(i):
+            g, j = group_of[i]
             nc.scalar.activation(
                 out=a_tiles[i][:],
                 in_=a_tiles[i][:],
@@ -249,6 +368,9 @@ def tile_memory_t_kernel(tc, key, memory, out):
                 bias=neg_max[g][:, j : j + 1],
                 accum_out=sums[g][:, j : j + 1],
             )
+
+        def normalise(i):
+            g, j = group_of[i]
             nc.vector.reciprocal(out=inv_sums[g][:, j : j + 1], in_=sums[g][:, j : j + 1])
             w_tiles[i] = w_pool.tile([P, N_PASSES, K_PASS], BF16, name="w_tile")
             nc.gpsimd.tensor_scalar(
@@ -261,102 +383,159 @@ def tile_memory_t_kernel(tc, key, memory, out):
             )
 
         def turn_w(i):
-            turned = turn_words(w_tiles[i][:])
-            w_grouped[i] = short.tile([P, N_PASSES, P, PACK], BF16, name="w_grouped", align_bytes=64)
-            nc.vector.tensor_copy(out=w_grouped[i][:].bitcast(F32), in_=turned[:].rearrange("p c u r -> p c r u"))
+            turn(("w", i), w_tiles[i][:])
 
-        def quantise_w(i):
-            w_codes[i] = w_pool.tile([P, N_PASSES * P], U32, name="w_codes", align_bytes=64)
-            w_scales[i] = w_pool.tile([P, N_PASSES * P], U8, name="w_scales", align_bytes=64)
-            nc.vector.quantize_mx(
-                out=w_codes[i][:].bitcast(FP8X4),
-                scales=w_scales[i][:],
-                in_=w_grouped[i][:].rearrange("p c r t -> p (c r t)"),
+        w_chunk = {}
+
+        def w_place(i, largest):
+            g, j = group_of[i]
+            for first, count in chunks(GROUP_SIZES[g], largest):
+                if first <= j < first + count:
+                    if (g, first) not in w_chunk:
+                        w_chunk[g, first] = grouped_tile([P, 4, N_PASSES, P, PACK])
+                    return w_chunk[g, first], j - first
+
+        def group_w(i, largest, engine=None):
+            rows, j = w_place(i, largest)
+            (engine or nc.vector.tensor_copy)(
+                out=rows[:, j, :, :, :].bitcast(F32), in_=turned["w", i][:].rearrange("p c u r -> p c r u")
             )
 
-        def second_matmul_and_store(i):
-            out_acc = out_psum.tile([P, D], F32, name="out_acc")
+        def quantise_w(g, j, count, largest):
+            if j == 0:
+                w_codes[g] = w_out.tile([P, max(GROUP_SIZES) * N_PASSES * P], U32, name="w_codes", align_bytes=64)
+                w_scales[g] = w_out.tile([P, max(GROUP_SIZES) * N_PASSES * P], U8, name="w_scales", align_bytes=64)
+            rows, at = w_place(first_of[g] + j, largest)
+            lo, hi = j * N_PASSES * P, (j + count) * N_PASSES * P
+            nc.vector.quantize_mx(
+                out=w_codes[g][:, lo:hi].bitcast(FP8X4),
+                scales=w_scales[g][:, lo:hi],
+                in_=rows[:, at : at + count, :, :, :].rearrange("p j c r t -> p (j c r t)"),
+            )
+
+        def second_matmul(i):
+            out_acc[i] = out_psum.tile([P, D], F32, name="out_acc")
+            g, j = group_of[i]
             for c in range(N_PASSES):
+                lo = (j * N_PASSES + c) * P
                 nc.tensor.matmul_mx(
-                    out=out_acc[:],
-                    lhsT=w_codes[i][:, c * P : (c + 1) * P].bitcast(FP8X4),
-                    lhsT_scale=w_scales[i][:, c * P : (c + 1) * P],
+                    out=out_acc[i][:],
+                    lhsT=w_codes[g][:, lo : lo + P].bitcast(FP8X4),
+                    lhsT_scale=w_scales[g][:, lo : lo + P],
                     rhs=m2_codes[:, c * D : (c + 1) * D].bitcast(FP8X4),
                     rhs_scale=m2_scales[:, c * D : (c + 1) * D],
                     start=(c == 0),
                     stop=(c == N_PASSES - 1),
                 )
-            out_sb = short.tile([P, D], F32, name="out_sb")
-            nc.scalar.copy(out=out_sb[:], in_=out_acc[:])
+
+        def store(i):
+            out_sb = out_pool.tile([P, D], F32, name="out_sb")
+            nc.scalar.copy(out=out_sb[:], in_=out_acc[i][:])
             nc.sync.dma_start(out=out_rows[:, i, :], in_=out_sb[:])
 
-        for i in range(DOTS_TILES):
-            first_matmul(i)
-        for g in range(GROUPS + 1):
-            here = g * GROUP
-            lo = here - GROUP
-            if g + 2 < GROUPS:
-                load_k(g + 2)
+        def k_steps(first, size):
+            pairs = list(range(first // 2, (first + size) // 2))
+            calls = []
+            for n in range(len(pairs) + 3):
+                for s, call in enumerate((turn_k, group_k, gram_k, sum_squares_k)):
+                    if 0 <= n - s < len(pairs):
+                        calls.append((call, pairs[n - s]))
+            return calls
 
-            if g < GROUPS:
-                for j in range(GROUP):
-                    scaled_dots(here + j)
-                for j in range(GROUP):
+        quantise_k(0)
+        first_matmuls()
+        k_rough = rough_inverse(k_sum_sq[0], GROUP_SIZES[0], "k_inv0")
+        k_scale[0] = newton(nc.gpsimd, k_sum_sq[0], k_rough, GROUP_SIZES[0], PI_2, "k_inv0")
+        for i in range(SCALED_AHEAD):
+            scaled_dots(i)
+
+        for g in range(groups):
+            size = GROUP_SIZES[g]
+            here = first_of[g]
+            last = first_of[g - 1] if g > 0 else None
+            last_size = GROUP_SIZES[g - 1] if g > 0 else 0
+            is_last = g + 1 == groups
+
+            calls = k_steps(first_of[g + 1], GROUP_SIZES[g + 1]) if not is_last else []
+            w_left = list(range(last_size))
+            steps = max(size, last_size)
+            share = -(-len(calls) // steps)
+            for j in range(steps):
+                if j < size:
                     sine(here + j)
-                for j in range(GROUP):
-                    square(here + j)
-            if g + 1 < GROUPS:
-                k_sum_sq[g + 1] = stat.tile([P, GROUP], F32, name="k_sum_sq")
-                for j in range(GROUP):
-                    sum_squares(k_sb[g + 1], k_sum_sq[g + 1], j)
-            if 0 < g < GROUPS:
-                for j in range(GROUP):
-                    turn_w(lo + j)
-            if g + 1 < GROUPS:
-                turn_k(g + 1)
+                    if SQUARES[g][j] == "G":
+                        square(here + j, "G")
+                if j < last_size:
+                    turn_w(last + j)
+                if j + SCALED_AHEAD < size:
+                    scaled_dots(here + j + SCALED_AHEAD)
+                if j < last_size:
+                    group_w(last + j, 4)
+                for call, q in calls[j * share : (j + 1) * share]:
+                    call(q)
+            for j in range(size):
+                if SQUARES[g][j] != "G":
+                    square(here + j, SQUARES[g][j])
             if g == 0:
-                for c in range(N_PASSES):
-                    nc.vector.tensor_copy(
-                        out=m2_grouped[:, c, :, :],
-                        in_=m_sb[:, c * PACK : (c + 1) * PACK, :].rearrange("p t d -> p d t"),
-                    )
                 nc.vector.quantize_mx(
                     out=m2_codes[:].bitcast(FP8X4),
                     scales=m2_scales[:],
                     in_=m2_grouped[:].rearrange("p c d t -> p (c d t)"),
                 )
-            if 0 < g < GROUPS:
-                for j in range(GROUP):
-                    quantise_w(lo + j)
-            if g + 1 < GROUPS:
+            if not is_last:
                 quantise_k(g + 1)
-                for i in range(DOTS_TILES):
-                    first_matmul(here + GROUP + i)
-            if g == GROUPS:
-                for j in range(GROUP + 3):
-                    if j < GROUP:
-                        turn_w(lo + j)
-                    if 1 <= j <= GROUP:
-                        quantise_w(lo + j - 1)
-                    if j >= 3:
-                        second_matmul_and_store(lo + j - 3)
+            for j, count in chunks(last_size, 4):
+                quantise_w(g - 1, j, count, 4)
+            if not is_last:
+                first_matmuls()
+            for j in range(min(OUT_BANKS, last_size)):
+                second_matmul(last + j)
 
-            if g + 1 < GROUPS:
-                k_scale[g + 1] = inverse_norm(k_sum_sq[g + 1], GROUP, PI_2, "k_inv")
-            if g < GROUPS:
-                for j in range(GROUP):
-                    inverse_cosine(here + j)
-                neg_max[g] = stat.tile([P, GROUP], F32, name="neg_max")
-                sums[g] = stat.tile([P, GROUP], F32, name="sums")
-                inv_sums[g] = stat.tile([P, GROUP], F32, name="inv_sums")
+            def outs(j):
+                if j < last_size:
+                    store(last + j)
+                    if j + OUT_BANKS < last_size:
+                        second_matmul(last + j + OUT_BANKS)
 
-            for j in range(GROUP + EXP_LAG):
-                if g < GROUPS and j < GROUP:
+            neg_max[g] = stat.tile([P, size], F32, name="neg_max%d" % g)
+            sums[g] = stat.tile([P, size], F32, name="sums%d" % g)
+            inv_sums[g] = stat.tile([P, size], F32, name="inv_sums%d" % g)
+            for j in range(size):
+                inverse_cosine(here + j)
+                if is_last and j < last_size:
+                    outs(j)
+                if j < TAN_AHEAD:
                     tangent(here + j)
-                if g < GROUPS and 1 <= j <= GROUP:
+                if 0 < j < TAN_AHEAD:
                     row_max(here + j - 1)
-                if j >= EXP_LAG:
-                    if g < GROUPS:
-                        softmax(here + j - EXP_LAG)
-                    if 0 < g < GROUPS:
-                        second_matmul_and_store(lo + j - EXP_LAG)
+            if is_last:
+                for j in range(size, last_size):
+                    outs(j)
+            if not is_last:
+                k_rough = rough_inverse(k_sum_sq[g + 1], GROUP_SIZES[g + 1], "k_inv%d" % (g + 1))
+                k_scale[g + 1] = newton(
+                    nc.gpsimd, k_sum_sq[g + 1], k_rough, GROUP_SIZES[g + 1], PI_2, "k_inv%d" % (g + 1)
+                )
+
+            for j in range(size + 1 if not is_last else size + LAGS[-1]):
+                if j < size:
+                    exponential(here + j)
+                if 0 < j <= size:
+                    normalise(here + j - 1)
+                n = j + TAN_AHEAD
+                if n < size:
+                    tangent(here + n)
+                if n <= size:
+                    row_max(here + n - 1)
+                if not is_last:
+                    outs(j)
+                    if j >= size - 1:
+                        for n in range(j + 1, last_size):
+                            outs(n)
+                n = j - (size - SCALED_AHEAD)
+                if not is_last and 0 <= n < SCALED_AHEAD:
+                    scaled_dots(first_of[g + 1] + n)
+                if is_last:
+                    for s, call in enumerate((turn_w, lambda i: group_w(i, 1), lambda i: quantise_w(g, i - here, 1, 1), second_matmul, store)):
+                        if 0 <= j - LAGS[s] < size:
+                            call(here + j - LAGS[s])

@@ -10,7 +10,6 @@ U8 = mybir.dt.uint8
 FP8X4 = mybir.dt.float8_e4m3fn_x4
 ACT = mybir.ActivationFunctionType
 ALU = mybir.AluOpType
-AXIS = mybir.AxisListType
 
 P = 128
 PACK = 4
@@ -28,9 +27,10 @@ TURN_BANKS = 3
 OUT_BANKS = 2
 SCALED_AHEAD = 3
 TAN_AHEAD = 4
+LAST_TAN_AHEAD = 6
 LAGS = (2, 2, 3, 4, 5)
-SQUARES = ["GGGGGSGS","GGGGGSGS","GGGGGSGS","GGGGGSGS"]
-VECTOR_NORMS = 3
+SQUARES = ["GGGGGGSS","GGGGGGSS","GGGGGGSS","GGGGGGSS"]
+VECTOR_NORMS = 0
 PI_2 = 3.14159 / 2
 EPS = 1e-8
 HUGE = 3.0e38
@@ -164,16 +164,17 @@ def tile_memory_t_kernel(tc, key, memory, out):
                 in_=turned["k", q][:].rearrange("p a u r -> p a r u"),
             )
 
-        def quantise_k(g):
+        def quantise_k(g, runs):
             size = GROUP_SIZES[g]
-            k_codes[g] = k_out.tile([P, max(GROUP_SIZES) * P], U32, name="k_codes", align_bytes=64)
-            k_scales[g] = k_out.tile([P, max(GROUP_SIZES) * P], U8, name="k_scales", align_bytes=64)
-            for j, count in chunks(size, 8):
+            if g not in k_codes:
+                k_codes[g] = k_out.tile([P, max(GROUP_SIZES) * P], U32, name="k_codes", align_bytes=64)
+                k_scales[g] = k_out.tile([P, max(GROUP_SIZES) * P], U8, name="k_scales", align_bytes=64)
+            for j, count in runs:
                 rows, at = k_place(first_of[g] + j)
                 nc.vector.quantize_mx(
                     out=k_codes[g][:, j * P : (j + count) * P].bitcast(FP8X4),
                     scales=k_scales[g][:, j * P : (j + count) * P],
-                    in_=rows[:, 0:count, :, :].rearrange("p a r t -> p (a r t)"),
+                    in_=rows[:, at : at + count, :, :].rearrange("p a r t -> p (a r t)"),
                 )
                 for n in range(j, j + count):
                     coded.append(first_of[g] + n)
@@ -210,20 +211,18 @@ def tile_memory_t_kernel(tc, key, memory, out):
 
         squares = keep.tile([P, 2, D], BF16, name="squares")
         m_sum_sq = keep.tile([P, N_BLOCKS], F32, name="m_sum_sq")
-        for j in range(VECTOR_NORMS, N_BLOCKS):
-            nc.scalar.activation(
-                out=squares[:, 0, :], in_=m_sb[:, j, :], func=ACT.Square, accum_out=m_sum_sq[:, j : j + 1]
-            )
-        for j in range(VECTOR_NORMS):
-            nc.vector.scalar_tensor_tensor(
-                out=squares[:, 1, :],
-                in0=m_sb[:, j, :],
-                scalar=1.0,
-                in1=m_sb[:, j, :],
-                op0=ALU.mult,
-                op1=ALU.mult,
-                accum_out=m_sum_sq[:, j : j + 1],
-            )
+        k_sum_sq[0] = stat.tile([P, GROUP_SIZES[0]], F32, name="k_sum_sq0")
+
+        def sum_squares(rows, accum, on_vector):
+            if on_vector:
+                nc.vector.scalar_tensor_tensor(
+                    out=squares[:, 1, :], in0=rows, scalar=1.0, in1=rows, op0=ALU.mult, op1=ALU.mult, accum_out=accum
+                )
+            else:
+                nc.scalar.activation(out=squares[:, 0, :], in_=rows, func=ACT.Square, accum_out=accum)
+
+        for j in range(N_BLOCKS):
+            sum_squares(m_sb[:, j, :], m_sum_sq[:, j : j + 1], j < VECTOR_NORMS)
         m_rough = rough_inverse(m_sum_sq, N_BLOCKS, "m_inv")
         m1_grouped = [grouped_tile([P, 2, P, 2, PACK]) for h in range(HALVES)]
         m1_codes = keep.tile([P, N], U32, name="m1_codes", align_bytes=64)
@@ -235,42 +234,39 @@ def tile_memory_t_kernel(tc, key, memory, out):
                 out=m1_grouped[h][:, half, :, :, :].bitcast(F32),
                 in_=turned["m", v][:].rearrange("p e u r -> p r e u"),
             )
+            if half == 1:
+                nc.vector.quantize_mx(
+                    out=m1_codes[:, h * BANK : (h + 1) * BANK].bitcast(FP8X4),
+                    scales=m1_scales[:, h * BANK : (h + 1) * BANK],
+                    in_=m1_grouped[h][:].rearrange("p v r e t -> p (v r e t)"),
+                )
         first_pairs = list(range(GROUP_SIZES[0] // 2))
-        m_inv = newton(nc.vector, m_sum_sq, m_rough, N_BLOCKS, 1.0, "m_inv")
-        for q in first_pairs:
+        for q in first_pairs[:2]:
             turn_k(q)
-            group_k(q, nc.scalar.copy if q < 2 else None)
-            if q == 1:
-                m_inv_all = keep.tile([P, N], F32, name="m_inv_all")
-                spreads = []
-                for h in range(HALVES):
-                    spread = dots_psum.tile([P, BANK], F32, name="spread", tag="dots")
-                    for a in range(BANK // P):
-                        j = h * (BANK // P) + a
-                        nc.tensor.matmul(
-                            out=spread[:, a * P : (a + 1) * P],
-                            lhsT=m_inv[:, j : j + 1].to_broadcast([P, P]),
-                            rhs=ident_f32[:],
-                            start=True,
-                            stop=True,
-                        )
-                    spreads.append(spread)
+            group_k(q)
+        m_inv = newton(nc.vector, m_sum_sq, m_rough, N_BLOCKS, 1.0, "m_inv")
+        quantise_k(0, ((0, 4),))
+        m_inv_all = keep.tile([P, N], F32, name="m_inv_all")
         for h in range(HALVES):
-            nc.vector.quantize_mx(
-                out=m1_codes[:, h * BANK : (h + 1) * BANK].bitcast(FP8X4),
-                scales=m1_scales[:, h * BANK : (h + 1) * BANK],
-                in_=m1_grouped[h][:].rearrange("p v r e t -> p (v r e t)"),
-            )
-        k_sum_sq[0] = stat.tile([P, GROUP_SIZES[0]], F32, name="k_sum_sq0")
-        for j in range(GROUP_SIZES[0]):
-            nc.scalar.activation(
-                out=squares[:, 0, :], in_=k_sb[j // 2][:, j % 2, :], func=ACT.Square, accum_out=k_sum_sq[0][:, j : j + 1]
-            )
-        for h in range(HALVES):
-            (nc.vector.tensor_copy, nc.vector.tensor_copy)[h](
+            spread = dots_psum.tile([P, BANK], F32, name="spread", tag="dots")
+            for a in range(BANK // P):
+                j = h * (BANK // P) + a
+                nc.tensor.transpose(
+                    out=spread[:, a * P : (a + 1) * P],
+                    in_=m_inv[:, j : j + 1].to_broadcast([P, P]),
+                    identity=ident_f32[:],
+                )
+            nc.vector.tensor_copy(
                 out=m_inv_all[:, h * BANK : (h + 1) * BANK].rearrange("p (u r e) -> p u r e", u=2, e=2),
-                in_=spreads[h][:].rearrange("p (u e r) -> p u r e", u=2, e=2),
+                in_=spread[:].rearrange("p (u e r) -> p u r e", u=2, e=2),
             )
+        for q in first_pairs[2:]:
+            turn_k(q)
+        for j in range(GROUP_SIZES[0]):
+            sum_squares(k_sb[j // 2][:, j % 2, :], k_sum_sq[0][:, j : j + 1], j < 0)
+        for q in first_pairs[2:]:
+            group_k(q, 0 and nc.scalar.copy)
+        quantise_k(0, ((4, 4),))
 
         m2_grouped = grouped_tile([P, N_PASSES, D, PACK])
         m2_codes = keep.tile([P, N_PASSES * D], U32, name="m2_codes", align_bytes=64)
@@ -285,6 +281,7 @@ def tile_memory_t_kernel(tc, key, memory, out):
                     op0=ALU.mult,
                     op1=ALU.add,
                 )
+        unread = keep.tile([P, 2, N], BF16, name="unread")
         dots = {}
         a_tiles = {}
         b_tiles = {}
@@ -355,8 +352,14 @@ def tile_memory_t_kernel(tc, key, memory, out):
 
         def row_max(i):
             g, j = group_of[i]
-            nc.vector.tensor_reduce(
-                out=neg_max[g][:, j : j + 1], in_=a_tiles[i][:], axis=AXIS.X, op=ALU.max, negate=True
+            nc.vector.tensor_scalar(
+                out=unread[:, i % 2, :],
+                in0=a_tiles[i][:],
+                scalar1=-1.0,
+                scalar2=None,
+                op0=ALU.mult,
+                op1=ALU.min,
+                accum_out=neg_max[g][:, j : j + 1],
             )
 
         def exponential(i):
@@ -369,11 +372,11 @@ def tile_memory_t_kernel(tc, key, memory, out):
                 accum_out=sums[g][:, j : j + 1],
             )
 
-        def normalise(i):
+        def normalise(i, engine=nc.gpsimd):
             g, j = group_of[i]
             nc.vector.reciprocal(out=inv_sums[g][:, j : j + 1], in_=sums[g][:, j : j + 1])
             w_tiles[i] = w_pool.tile([P, N_PASSES, K_PASS], BF16, name="w_tile")
-            nc.gpsimd.tensor_scalar(
+            engine.tensor_scalar(
                 out=w_tiles[i][:].rearrange("p c f -> p (c f)"),
                 in0=a_tiles[i][:],
                 scalar1=inv_sums[g][:, j : j + 1],
@@ -442,7 +445,6 @@ def tile_memory_t_kernel(tc, key, memory, out):
                         calls.append((call, pairs[n - s]))
             return calls
 
-        quantise_k(0)
         first_matmuls()
         k_rough = rough_inverse(k_sum_sq[0], GROUP_SIZES[0], "k_inv0")
         k_scale[0] = newton(nc.gpsimd, k_sum_sq[0], k_rough, GROUP_SIZES[0], PI_2, "k_inv0")
@@ -483,7 +485,7 @@ def tile_memory_t_kernel(tc, key, memory, out):
                     in_=m2_grouped[:].rearrange("p c d t -> p (c d t)"),
                 )
             if not is_last:
-                quantise_k(g + 1)
+                quantise_k(g + 1, chunks(GROUP_SIZES[g + 1], 8))
             for j, count in chunks(last_size, 4):
                 quantise_w(g - 1, j, count, 4)
             if not is_last:
@@ -500,13 +502,14 @@ def tile_memory_t_kernel(tc, key, memory, out):
             neg_max[g] = stat.tile([P, size], F32, name="neg_max%d" % g)
             sums[g] = stat.tile([P, size], F32, name="sums%d" % g)
             inv_sums[g] = stat.tile([P, size], F32, name="inv_sums%d" % g)
+            ahead = LAST_TAN_AHEAD if is_last else TAN_AHEAD
             for j in range(size):
                 inverse_cosine(here + j)
                 if is_last and j < last_size:
                     outs(j)
-                if j < TAN_AHEAD:
+                if j < ahead:
                     tangent(here + j)
-                if 0 < j < TAN_AHEAD:
+                if 0 < j < ahead:
                     row_max(here + j - 1)
             if is_last:
                 for j in range(size, last_size):
@@ -520,13 +523,15 @@ def tile_memory_t_kernel(tc, key, memory, out):
             for j in range(size + 1 if not is_last else size + LAGS[-1]):
                 if j < size:
                     exponential(here + j)
-                if 0 < j <= size:
+                n = j + ahead
+                if 0 < j <= size and not is_last:
                     normalise(here + j - 1)
-                n = j + TAN_AHEAD
                 if n < size:
                     tangent(here + n)
                 if n <= size:
                     row_max(here + n - 1)
+                if 0 < j <= size and is_last:
+                    normalise(here + j - 1, nc.vector)
                 if not is_last:
                     outs(j)
                     if j >= size - 1:

@@ -29,7 +29,7 @@ SCALED_AHEAD = 3
 TAN_AHEAD = 4
 LAST_TAN_AHEAD = 6
 LAGS = (2, 2, 3, 4, 5)
-SQUARES = ["GGGGGGSS","GGGGGGSS","GGGGGGSS","GGGGGGSS"]
+SQUARES = ["GGGGGGSS","GGGGGGSS","GGGGGGSS","GVGVGSGS"]
 VECTOR_NORMS = 0
 PI_2 = 3.14159 / 2
 EPS = 1e-8
@@ -197,8 +197,6 @@ def tile_memory_t_kernel(tc, key, memory, out):
         def sum_squares_k(q):
             for a in range(2):
                 g, j = group_of[2 * q + a]
-                if j == 0:
-                    k_sum_sq[g] = stat.tile([P, GROUP_SIZES[g]], F32, name="k_sum_sq%d" % g)
                 nc.vector.scalar_tensor_tensor(
                     out=diag[:],
                     in0=gram[q][:, a, :],
@@ -436,14 +434,30 @@ def tile_memory_t_kernel(tc, key, memory, out):
             nc.scalar.copy(out=out_sb[:], in_=out_acc[i][:])
             nc.sync.dma_start(out=out_rows[:, i, :], in_=out_sb[:])
 
-        def k_steps(first, size):
-            pairs = list(range(first // 2, (first + size) // 2))
-            calls = []
-            for n in range(len(pairs) + 3):
-                for s, call in enumerate((turn_k, group_k, gram_k, sum_squares_k)):
-                    if 0 <= n - s < len(pairs):
-                        calls.append((call, pairs[n - s]))
-            return calls
+        GRAM_STEPS = (3, 5, 7, 8)
+        SUM_STEPS = (6, 8, 10, 12)
+
+        NORMS = "PSPS"
+        NORM_STEPS = (1, 3, 5, 7)
+
+        def k_step(g, step):
+            pairs = list(range(first_of[g] // 2, (first_of[g] + GROUP_SIZES[g]) // 2))
+            for n, q in enumerate(pairs):
+                if step == n + 1:
+                    group_k(q)
+                if step == n:
+                    turn_k(q)
+                if step == 0 and n == 0:
+                    k_sum_sq[g] = stat.tile([P, GROUP_SIZES[g]], F32, name="k_sum_sq%d" % g)
+                if NORMS[n] == "P":
+                    if step == GRAM_STEPS[n]:
+                        gram_k(q)
+                    if step == SUM_STEPS[n]:
+                        sum_squares_k(q)
+                elif step == NORM_STEPS[n]:
+                    for a in range(2):
+                        j = 2 * n + a
+                        sum_squares(k_sb[q][:, a, :], k_sum_sq[g][:, j : j + 1], NORMS[n] == "V")
 
         first_matmuls()
         k_rough = rough_inverse(k_sum_sq[0], GROUP_SIZES[0], "k_inv0")
@@ -458,10 +472,8 @@ def tile_memory_t_kernel(tc, key, memory, out):
             last_size = GROUP_SIZES[g - 1] if g > 0 else 0
             is_last = g + 1 == groups
 
-            calls = k_steps(first_of[g + 1], GROUP_SIZES[g + 1]) if not is_last else []
             w_left = list(range(last_size))
             steps = max(size, last_size)
-            share = -(-len(calls) // steps)
             for j in range(steps):
                 if j < size:
                     sine(here + j)
@@ -473,8 +485,8 @@ def tile_memory_t_kernel(tc, key, memory, out):
                     scaled_dots(here + j + SCALED_AHEAD)
                 if j < last_size:
                     group_w(last + j, 4)
-                for call, q in calls[j * share : (j + 1) * share]:
-                    call(q)
+                if not is_last:
+                    k_step(g + 1, j)
             for j in range(size):
                 if SQUARES[g][j] != "G":
                     square(here + j, SQUARES[g][j])
@@ -511,6 +523,8 @@ def tile_memory_t_kernel(tc, key, memory, out):
                     tangent(here + j)
                 if 0 < j < ahead:
                     row_max(here + j - 1)
+                if not is_last:
+                    k_step(g + 1, steps + j)
             if is_last:
                 for j in range(size, last_size):
                     outs(j)

@@ -29,7 +29,7 @@ SCALED_AHEAD = 3
 TAN_AHEAD = 4
 LAST_TAN_AHEAD = 6
 LAGS = (2, 2, 3, 4, 5)
-SQUARES = ["GGGGGGSS","GGGGGGSS","GGGGGGSS","GVGVGSGS"]
+SQUARES = ["GVGVGVVS","GGGGGGSS","GGGGGGSS","GVGVGSGS"]
 VECTOR_NORMS = 0
 PI_2 = 3.14159 / 2
 EPS = 1e-8
@@ -53,7 +53,7 @@ def tile_memory_t_kernel(tc, key, memory, out):
         w_out = stack.enter_context(tc.tile_pool(name="w_out", bufs=1))
         stat = stack.enter_context(tc.tile_pool(name="stat", bufs=1))
         a_pool = stack.enter_context(tc.tile_pool(name="a_pool", bufs=max(GROUP_SIZES) + SCALED_AHEAD))
-        b_pool = stack.enter_context(tc.tile_pool(name="b_pool", bufs=max(GROUP_SIZES)))
+        b_pool = stack.enter_context(tc.tile_pool(name="b_pool", bufs=8))
         w_pool = stack.enter_context(tc.tile_pool(name="w_pool", bufs=9))
         out_pool = stack.enter_context(tc.tile_pool(name="out_pool", bufs=3))
         dots_psum = stack.enter_context(tc.psum_pool(name="dots_psum", bufs=DOTS_BANKS))
@@ -232,19 +232,13 @@ def tile_memory_t_kernel(tc, key, memory, out):
                 out=m1_grouped[h][:, half, :, :, :].bitcast(F32),
                 in_=turned["m", v][:].rearrange("p e u r -> p r e u"),
             )
-            if half == 1:
-                nc.vector.quantize_mx(
-                    out=m1_codes[:, h * BANK : (h + 1) * BANK].bitcast(FP8X4),
-                    scales=m1_scales[:, h * BANK : (h + 1) * BANK],
-                    in_=m1_grouped[h][:].rearrange("p v r e t -> p (v r e t)"),
-                )
         first_pairs = list(range(GROUP_SIZES[0] // 2))
-        for q in first_pairs[:2]:
+        for q in first_pairs:
             turn_k(q)
-            group_k(q)
+            group_k(q, None)
         m_inv = newton(nc.vector, m_sum_sq, m_rough, N_BLOCKS, 1.0, "m_inv")
-        quantise_k(0, ((0, 4),))
         m_inv_all = keep.tile([P, N], F32, name="m_inv_all")
+        spreads = []
         for h in range(HALVES):
             spread = dots_psum.tile([P, BANK], F32, name="spread", tag="dots")
             for a in range(BANK // P):
@@ -254,17 +248,21 @@ def tile_memory_t_kernel(tc, key, memory, out):
                     in_=m_inv[:, j : j + 1].to_broadcast([P, P]),
                     identity=ident_f32[:],
                 )
+            spreads.append(spread)
+        for h in range(HALVES):
+            nc.vector.quantize_mx(
+                out=m1_codes[:, h * BANK : (h + 1) * BANK].bitcast(FP8X4),
+                scales=m1_scales[:, h * BANK : (h + 1) * BANK],
+                in_=m1_grouped[h][:].rearrange("p v r e t -> p (v r e t)"),
+            )
+        quantise_k(0, chunks(GROUP_SIZES[0], 8))
+        for h in range(HALVES):
             nc.vector.tensor_copy(
                 out=m_inv_all[:, h * BANK : (h + 1) * BANK].rearrange("p (u r e) -> p u r e", u=2, e=2),
-                in_=spread[:].rearrange("p (u e r) -> p u r e", u=2, e=2),
+                in_=spreads[h][:].rearrange("p (u e r) -> p u r e", u=2, e=2),
             )
-        for q in first_pairs[2:]:
-            turn_k(q)
         for j in range(GROUP_SIZES[0]):
             sum_squares(k_sb[j // 2][:, j % 2, :], k_sum_sq[0][:, j : j + 1], j < 0)
-        for q in first_pairs[2:]:
-            group_k(q, 0 and nc.scalar.copy)
-        quantise_k(0, ((4, 4),))
 
         m2_grouped = grouped_tile([P, N_PASSES, D, PACK])
         m2_codes = keep.tile([P, N_PASSES * D], U32, name="m2_codes", align_bytes=64)
@@ -279,7 +277,7 @@ def tile_memory_t_kernel(tc, key, memory, out):
                     op0=ALU.mult,
                     op1=ALU.add,
                 )
-        unread = keep.tile([P, 2, N], BF16, name="unread")
+        unread = keep.tile([P, 1, N], BF16, name="unread")
         dots = {}
         a_tiles = {}
         b_tiles = {}
@@ -351,7 +349,7 @@ def tile_memory_t_kernel(tc, key, memory, out):
         def row_max(i):
             g, j = group_of[i]
             nc.vector.tensor_scalar(
-                out=unread[:, i % 2, :],
+                out=unread[:, 0, :],
                 in0=a_tiles[i][:],
                 scalar1=-1.0,
                 scalar2=None,
@@ -434,11 +432,6 @@ def tile_memory_t_kernel(tc, key, memory, out):
             nc.scalar.copy(out=out_sb[:], in_=out_acc[i][:])
             nc.sync.dma_start(out=out_rows[:, i, :], in_=out_sb[:])
 
-        GRAM_STEPS = (3, 5, 7, 8)
-        SUM_STEPS = (6, 8, 10, 12)
-
-        NORMS = "PSPS"
-        NORM_STEPS = (1, 3, 5, 7)
 
         def k_step(g, step):
             pairs = list(range(first_of[g] // 2, (first_of[g] + GROUP_SIZES[g]) // 2))
@@ -449,15 +442,15 @@ def tile_memory_t_kernel(tc, key, memory, out):
                     turn_k(q)
                 if step == 0 and n == 0:
                     k_sum_sq[g] = stat.tile([P, GROUP_SIZES[g]], F32, name="k_sum_sq%d" % g)
-                if NORMS[n] == "P":
-                    if step == GRAM_STEPS[n]:
+                if n % 2 == 0:
+                    if step == 2 * n + 3:
                         gram_k(q)
-                    if step == SUM_STEPS[n]:
+                    if step == 2 * n + 6:
                         sum_squares_k(q)
-                elif step == NORM_STEPS[n]:
+                elif step == 2 * n + 1:
                     for a in range(2):
                         j = 2 * n + a
-                        sum_squares(k_sb[q][:, a, :], k_sum_sq[g][:, j : j + 1], NORMS[n] == "V")
+                        sum_squares(k_sb[q][:, a, :], k_sum_sq[g][:, j : j + 1], False)
 
         first_matmuls()
         k_rough = rough_inverse(k_sum_sq[0], GROUP_SIZES[0], "k_inv0")
@@ -488,7 +481,7 @@ def tile_memory_t_kernel(tc, key, memory, out):
                 if not is_last:
                     k_step(g + 1, j)
             for j in range(size):
-                if SQUARES[g][j] != "G":
+                if SQUARES[g][j] in "SV":
                     square(here + j, SQUARES[g][j])
             if g == 0:
                 nc.vector.quantize_mx(
@@ -517,8 +510,10 @@ def tile_memory_t_kernel(tc, key, memory, out):
             ahead = LAST_TAN_AHEAD if is_last else TAN_AHEAD
             for j in range(size):
                 inverse_cosine(here + j)
-                if is_last and j < last_size:
-                    outs(j)
+                if j + 4 < size and SQUARES[g][j + 4] == "R":
+                    square(here + j + 4, "S")
+                if (is_last or j >= size - 2) and j < last_size:
+                    outs(j if is_last else j - size + 2)
                 if j < ahead:
                     tangent(here + j)
                 if 0 < j < ahead:
@@ -545,12 +540,9 @@ def tile_memory_t_kernel(tc, key, memory, out):
                 if n <= size:
                     row_max(here + n - 1)
                 if 0 < j <= size and is_last:
-                    normalise(here + j - 1, nc.vector)
-                if not is_last:
-                    outs(j)
-                    if j >= size - 1:
-                        for n in range(j + 1, last_size):
-                            outs(n)
+                    normalise(here + j - 1)
+                if not is_last and j + 2 < last_size:
+                    outs(j + 2)
                 n = j - (size - SCALED_AHEAD)
                 if not is_last and 0 <= n < SCALED_AHEAD:
                     scaled_dots(first_of[g + 1] + n)

@@ -25,11 +25,11 @@ HALVES = N // BANK
 DOTS_BANKS = 3
 TURN_BANKS = 3
 OUT_BANKS = 2
-SCALED_AHEAD = 3
-TAN_AHEAD = 4
-LAST_TAN_AHEAD = 6
-LAGS = (2, 2, 3, 4, 5)
-SQUARES = ["GVGVGVVS","GGGGGGSS","GGGGGGSS","GVGVGSGS"]
+SCALED_AHEAD = 4
+TAN_AHEAD = 5
+LAST_TAN_AHEAD = 5
+LAGS = (2, 3, 4, 5, 6)
+SQUARES = ["GGVGGVGS","GGGGGSSS","GGGGGSSS","GGGGSSSS"]
 VECTOR_NORMS = 0
 PI_2 = 3.14159 / 2
 EPS = 1e-8
@@ -49,13 +49,13 @@ def tile_memory_t_kernel(tc, key, memory, out):
         keep = stack.enter_context(tc.tile_pool(name="keep", bufs=1))
         k_in = stack.enter_context(tc.tile_pool(name="k_in", bufs=6))
         k_out = stack.enter_context(tc.tile_pool(name="k_out", bufs=2))
-        grouped_pool = stack.enter_context(tc.tile_pool(name="grouped_pool", bufs=7))
+        grouped_pool = stack.enter_context(tc.tile_pool(name="grouped_pool", bufs=6))
         w_out = stack.enter_context(tc.tile_pool(name="w_out", bufs=1))
         stat = stack.enter_context(tc.tile_pool(name="stat", bufs=1))
         a_pool = stack.enter_context(tc.tile_pool(name="a_pool", bufs=max(GROUP_SIZES) + SCALED_AHEAD))
         b_pool = stack.enter_context(tc.tile_pool(name="b_pool", bufs=8))
         w_pool = stack.enter_context(tc.tile_pool(name="w_pool", bufs=9))
-        out_pool = stack.enter_context(tc.tile_pool(name="out_pool", bufs=3))
+        out_pool = stack.enter_context(tc.tile_pool(name="out_pool", bufs=5))
         dots_psum = stack.enter_context(tc.psum_pool(name="dots_psum", bufs=DOTS_BANKS))
         turn_psum = stack.enter_context(tc.psum_pool(name="turn_psum", bufs=TURN_BANKS))
         out_psum = stack.enter_context(tc.psum_pool(name="out_psum", bufs=OUT_BANKS))
@@ -235,7 +235,7 @@ def tile_memory_t_kernel(tc, key, memory, out):
         first_pairs = list(range(GROUP_SIZES[0] // 2))
         for q in first_pairs:
             turn_k(q)
-            group_k(q, None)
+            group_k(q, nc.scalar.copy if q >= 3 else None)
         m_inv = newton(nc.vector, m_sum_sq, m_rough, N_BLOCKS, 1.0, "m_inv")
         m_inv_all = keep.tile([P, N], F32, name="m_inv_all")
         spreads = []
@@ -445,9 +445,9 @@ def tile_memory_t_kernel(tc, key, memory, out):
                 if n % 2 == 0:
                     if step == 2 * n + 3:
                         gram_k(q)
-                    if step == 2 * n + 6:
+                    if step == 2 * n + 5:
                         sum_squares_k(q)
-                elif step == 2 * n + 1:
+                elif step == 2 * n + 3:
                     for a in range(2):
                         j = 2 * n + a
                         sum_squares(k_sb[q][:, a, :], k_sum_sq[g][:, j : j + 1], False)
@@ -512,8 +512,8 @@ def tile_memory_t_kernel(tc, key, memory, out):
                 inverse_cosine(here + j)
                 if j + 4 < size and SQUARES[g][j + 4] == "R":
                     square(here + j + 4, "S")
-                if (is_last or j >= size - 2) and j < last_size:
-                    outs(j if is_last else j - size + 2)
+                if (is_last or j >= size - 1) and j < last_size:
+                    outs(j if is_last else j - size + 1)
                 if j < ahead:
                     tangent(here + j)
                 if 0 < j < ahead:
@@ -534,15 +534,15 @@ def tile_memory_t_kernel(tc, key, memory, out):
                     exponential(here + j)
                 n = j + ahead
                 if 0 < j <= size and not is_last:
-                    normalise(here + j - 1)
+                    normalise(here + j - 1, nc.vector if "GGGGGGGG"[j - 1] == "V" else nc.gpsimd)
                 if n < size:
                     tangent(here + n)
                 if n <= size:
                     row_max(here + n - 1)
                 if 0 < j <= size and is_last:
-                    normalise(here + j - 1)
-                if not is_last and j + 2 < last_size:
-                    outs(j + 2)
+                    normalise(here + j - 1, nc.vector if "GGGGGGGG"[j - 1] == "V" else nc.gpsimd)
+                if not is_last and j + 1 < last_size:
+                    outs(j + 1)
                 n = j - (size - SCALED_AHEAD)
                 if not is_last and 0 <= n < SCALED_AHEAD:
                     scaled_dots(first_of[g + 1] + n)

@@ -22,14 +22,14 @@ N_BLOCKS = N // P
 N_PASSES = N // K_PASS
 BANK = 512
 HALVES = N // BANK
-DOTS_BANKS = 3
-TURN_BANKS = 3
+DOTS_BANKS = 2
+TURN_BANKS = 4
 OUT_BANKS = 2
 SCALED_AHEAD = 4
 TAN_AHEAD = 5
 LAST_TAN_AHEAD = 5
 LAGS = (2, 3, 4, 5, 6)
-SQUARES = ["GGVGGVGS","GGGGGSSS","GGGGGSSS","GGGGSSSS"]
+SQUARES = ["GGVGGVGS","GGGGGSSS","GGGGGSSS","GVGVGVSS"]
 VECTOR_NORMS = 0
 PI_2 = 3.14159 / 2
 EPS = 1e-8
@@ -143,7 +143,7 @@ def tile_memory_t_kernel(tc, key, memory, out):
         k_sum_sq = {}
         k_scale = {}
         coded = []
-        diag = keep.tile([P, P], BF16, name="diag")
+        diag = keep.tile([P, 2, P], BF16, name="diag")
 
         def k_place(i):
             g, j = group_of[i]
@@ -198,7 +198,7 @@ def tile_memory_t_kernel(tc, key, memory, out):
             for a in range(2):
                 g, j = group_of[2 * q + a]
                 nc.vector.scalar_tensor_tensor(
-                    out=diag[:],
+                    out=diag[:, a, :],
                     in0=gram[q][:, a, :],
                     scalar=1.0,
                     in1=ident_f32[:],
@@ -235,7 +235,7 @@ def tile_memory_t_kernel(tc, key, memory, out):
         first_pairs = list(range(GROUP_SIZES[0] // 2))
         for q in first_pairs:
             turn_k(q)
-            group_k(q, nc.scalar.copy if q >= 3 else None)
+            group_k(q, None)
         m_inv = newton(nc.vector, m_sum_sq, m_rough, N_BLOCKS, 1.0, "m_inv")
         m_inv_all = keep.tile([P, N], F32, name="m_inv_all")
         spreads = []
@@ -443,7 +443,7 @@ def tile_memory_t_kernel(tc, key, memory, out):
                 if step == 0 and n == 0:
                     k_sum_sq[g] = stat.tile([P, GROUP_SIZES[g]], F32, name="k_sum_sq%d" % g)
                 if n % 2 == 0:
-                    if step == 2 * n + 3:
+                    if step == 2 * n + 4:
                         gram_k(q)
                     if step == 2 * n + 5:
                         sum_squares_k(q)
@@ -540,7 +540,7 @@ def tile_memory_t_kernel(tc, key, memory, out):
                 if n <= size:
                     row_max(here + n - 1)
                 if 0 < j <= size and is_last:
-                    normalise(here + j - 1, nc.vector if "GGGGGGGG"[j - 1] == "V" else nc.gpsimd)
+                    normalise(here + j - 1, nc.vector if "GGGGVVVV"[j - 1] == "V" else nc.gpsimd)
                 if not is_last and j + 1 < last_size:
                     outs(j + 1)
                 n = j - (size - SCALED_AHEAD)

@@ -207,17 +207,18 @@ def tile_memory_t_kernel(tc, key, memory, out):
                     accum_out=k_sum_sq[g][:, j : j + 1],
                 )
 
-        squares = keep.tile([P, 2, D], BF16, name="squares")
+        squares_pool = stack.enter_context(tc.tile_pool(name="squares_pool", bufs=3))
         m_sum_sq = keep.tile([P, N_BLOCKS], F32, name="m_sum_sq")
         k_sum_sq[0] = stat.tile([P, GROUP_SIZES[0]], F32, name="k_sum_sq0")
 
         def sum_squares(rows, accum, on_vector):
+            squares = squares_pool.tile([P, D], BF16, name="squares")
             if on_vector:
                 nc.vector.scalar_tensor_tensor(
-                    out=squares[:, 1, :], in0=rows, scalar=1.0, in1=rows, op0=ALU.mult, op1=ALU.mult, accum_out=accum
+                    out=squares[:], in0=rows, scalar=1.0, in1=rows, op0=ALU.mult, op1=ALU.mult, accum_out=accum
                 )
             else:
-                nc.scalar.activation(out=squares[:, 0, :], in_=rows, func=ACT.Square, accum_out=accum)
+                nc.scalar.activation(out=squares[:], in_=rows, func=ACT.Square, accum_out=accum)
 
         for j in range(N_BLOCKS):
             sum_squares(m_sb[:, j, :], m_sum_sq[:, j : j + 1], j < VECTOR_NORMS)

@@ -29,11 +29,11 @@ SCALED_AHEAD = 4
 TAN_AHEAD = 5
 LAST_TAN_AHEAD = 5
 LAGS = (2, 3, 4, 5, 6)
-SQUARES = ["GGVGGVGS","GGGGGSSS","GGGGGSSS","GVGVGVSS"]
+SQUARES = ["GGSGSGSG","GGSGSGSG","GGSGSGSG","GGSGSGSG"]
 VECTOR_NORMS = 0
 PI_2 = 3.14159 / 2
 EPS = 1e-8
-HUGE = 3.0e38
+HUGE = 4096.0
 
 FLOPS = 2 * B * N * D * 2
 
@@ -55,6 +55,7 @@ def tile_memory_t_kernel(tc, key, memory, out):
         a_pool = stack.enter_context(tc.tile_pool(name="a_pool", bufs=max(GROUP_SIZES) + SCALED_AHEAD))
         b_pool = stack.enter_context(tc.tile_pool(name="b_pool", bufs=8))
         w_pool = stack.enter_context(tc.tile_pool(name="w_pool", bufs=9))
+        fold_pool = stack.enter_context(tc.tile_pool(name="fold_pool", bufs=2))
         out_pool = stack.enter_context(tc.tile_pool(name="out_pool", bufs=5))
         dots_psum = stack.enter_context(tc.psum_pool(name="dots_psum", bufs=DOTS_BANKS))
         turn_psum = stack.enter_context(tc.psum_pool(name="turn_psum", bufs=TURN_BANKS))
@@ -347,8 +348,23 @@ def tile_memory_t_kernel(tc, key, memory, out):
                 out=a_tiles[i][:], in0=b_tiles[i][:], scalar=HUGE, in1=a_tiles[i][:], op0=ALU.min, op1=ALU.mult
             )
 
-        def row_max(i):
+        def row_max(i, folded=False):
             g, j = group_of[i]
+            if folded:
+                fold = fold_pool.tile([P, BANK], BF16, name="fold")
+                nc.vector.tensor_tensor(
+                    out=fold[:], in0=a_tiles[i][:, 0:BANK], in1=a_tiles[i][:, BANK:N], op=ALU.max
+                )
+                nc.vector.tensor_scalar(
+                    out=unread[:, 0, 0:BANK],
+                    in0=fold[:],
+                    scalar1=-1.0,
+                    scalar2=None,
+                    op0=ALU.mult,
+                    op1=ALU.min,
+                    accum_out=neg_max[g][:, j : j + 1],
+                )
+                return
             nc.vector.tensor_scalar(
                 out=unread[:, 0, :],
                 in0=a_tiles[i][:],
@@ -414,8 +430,11 @@ def tile_memory_t_kernel(tc, key, memory, out):
             )
 
         def second_matmul(i):
-            out_acc[i] = out_psum.tile([P, D], F32, name="out_acc")
             g, j = group_of[i]
+            if g == groups - 1 and j % 4 >= 2:
+                out_acc[i] = dots_psum.tile([P, D], F32, name="out_acc", tag="dots")
+            else:
+                out_acc[i] = out_psum.tile([P, D], F32, name="out_acc")
             for c in range(N_PASSES):
                 lo = (j * N_PASSES + c) * P
                 nc.tensor.matmul_mx(
@@ -443,15 +462,10 @@ def tile_memory_t_kernel(tc, key, memory, out):
                     turn_k(q)
                 if step == 0 and n == 0:
                     k_sum_sq[g] = stat.tile([P, GROUP_SIZES[g]], F32, name="k_sum_sq%d" % g)
-                if n % 2 == 0:
-                    if step == 2 * n + 4:
-                        gram_k(q)
-                    if step == 2 * n + 5:
-                        sum_squares_k(q)
-                elif step == 2 * n + 3:
-                    for a in range(2):
-                        j = 2 * n + a
-                        sum_squares(k_sb[q][:, a, :], k_sum_sq[g][:, j : j + 1], False)
+                if step == n + 5:
+                    gram_k(q)
+                if step == n + 6:
+                    sum_squares_k(q)
 
         first_matmuls()
         k_rough = rough_inverse(k_sum_sq[0], GROUP_SIZES[0], "k_inv0")
@@ -473,6 +487,8 @@ def tile_memory_t_kernel(tc, key, memory, out):
                     sine(here + j)
                     if SQUARES[g][j] == "G":
                         square(here + j, "G")
+                    if j > 0 and SQUARES[g][j - 1] == "S":
+                        square(here + j - 1, "S")
                 if j < last_size:
                     turn_w(last + j)
                 if j + SCALED_AHEAD < size:
@@ -482,7 +498,7 @@ def tile_memory_t_kernel(tc, key, memory, out):
                 if not is_last:
                     k_step(g + 1, j)
             for j in range(size):
-                if SQUARES[g][j] in "SV":
+                if SQUARES[g][j] == "V" or SQUARES[g][j] == "S" and j == size - 1:
                     square(here + j, SQUARES[g][j])
             if g == 0:
                 nc.vector.quantize_mx(
@@ -518,7 +534,7 @@ def tile_memory_t_kernel(tc, key, memory, out):
                 if j < ahead:
                     tangent(here + j)
                 if 0 < j < ahead:
-                    row_max(here + j - 1)
+                    row_max(here + j - 1, True)
                 if not is_last:
                     k_step(g + 1, steps + j)
             if is_last:
@@ -548,6 +564,6 @@ def tile_memory_t_kernel(tc, key, memory, out):
                 if not is_last and 0 <= n < SCALED_AHEAD:
                     scaled_dots(first_of[g + 1] + n)
                 if is_last:
-                    for s, call in enumerate((turn_w, lambda i: group_w(i, 1), lambda i: quantise_w(g, i - here, 1, 1), second_matmul, store)):
+                    for s, call in enumerate((turn_w, lambda i: group_w(i, 1, nc.scalar.copy if "VVVVSSSS"[i - here] == "S" else nc.vector.tensor_copy), lambda i: quantise_w(g, i - here, 1, 1), second_matmul, store)):
                         if 0 <= j - LAGS[s] < size:
                             call(here + j - LAGS[s])

@@ -100,8 +100,9 @@ def tile_memory_t_kernel(tc, key, memory, out):
         nc.scalar.activation(out=one[:], in_=one[:], func=ACT.Abs_reciprocal_sqrt)
 
         m_sb = keep.tile([P, N_BLOCKS, D], BF16, name="m_sb")
-        for c in range(N_PASSES):
-            nc.sync.dma_start(out=m_sb[:, c * PACK : (c + 1) * PACK, :], in_=mem_rows[:, c, :, :])
+        for v in range(N_BLOCKS // 2):
+            c, half = divmod(v, 2)
+            nc.sync.dma_start(out=m_sb[:, 2 * v : 2 * v + 2, :], in_=mem_rows[:, c, 2 * half : 2 * half + 2, :])
 
         k_sb = {}
         loads = list(range(PAIRS))
@@ -462,10 +463,15 @@ def tile_memory_t_kernel(tc, key, memory, out):
                     turn_k(q)
                 if step == 0 and n == 0:
                     k_sum_sq[g] = stat.tile([P, GROUP_SIZES[g]], F32, name="k_sum_sq%d" % g)
-                if step == n + 5:
-                    gram_k(q)
-                if step == n + 6:
-                    sum_squares_k(q)
+                if n != 3:
+                    if step == n + 5:
+                        gram_k(q)
+                    if step == n + 6:
+                        sum_squares_k(q)
+                elif step == n + 5:
+                    for a in range(2):
+                        j = 2 * n + a
+                        sum_squares(k_sb[q][:, a, :], k_sum_sq[g][:, j : j + 1], False)
 
         first_matmuls()
         k_rough = rough_inverse(k_sum_sq[0], GROUP_SIZES[0], "k_inv0")
@@ -534,7 +540,7 @@ def tile_memory_t_kernel(tc, key, memory, out):
                 if j < ahead:
                     tangent(here + j)
                 if 0 < j < ahead:
-                    row_max(here + j - 1, True)
+                    row_max(here + j - 1)
                 if not is_last:
                     k_step(g + 1, steps + j)
             if is_last:

@@ -25,11 +25,11 @@ HALVES = N // BANK
 DOTS_BANKS = 2
 TURN_BANKS = 4
 OUT_BANKS = 2
-SCALED_AHEAD = 4
-TAN_AHEAD = 5
+SCALED_AHEAD = 3
+TAN_AHEAD = 4
 LAST_TAN_AHEAD = 5
 LAGS = (2, 3, 4, 5, 6)
-SQUARES = ["GGSGSGSG","GGSGSGSG","GGSGSGSG","GGSGSGSG"]
+SQUARES = ["GGSGSGSG","GGSGSGSG","GGSGSGSG","SGSGSGSG"]
 VECTOR_NORMS = 0
 PI_2 = 3.14159 / 2
 EPS = 1e-8
@@ -540,7 +540,7 @@ def tile_memory_t_kernel(tc, key, memory, out):
                 if j < ahead:
                     tangent(here + j)
                 if 0 < j < ahead:
-                    row_max(here + j - 1)
+                    row_max(here + j - 1, True)
                 if not is_last:
                     k_step(g + 1, steps + j)
             if is_last:
@@ -563,7 +563,7 @@ def tile_memory_t_kernel(tc, key, memory, out):
                 if n <= size:
                     row_max(here + n - 1)
                 if 0 < j <= size and is_last:
-                    normalise(here + j - 1, nc.vector if "GGGGVVVV"[j - 1] == "V" else nc.gpsimd)
+                    normalise(here + j - 1, nc.vector if "GGGVVVVV"[j - 1] == "V" else nc.gpsimd)
                 if not is_last and j + 1 < last_size:
                     outs(j + 1)
                 n = j - (size - SCALED_AHEAD)

@@ -26,11 +26,11 @@ DOTS_BANKS = 2
 TURN_BANKS = 4
 OUT_BANKS = 2
 SCALED_AHEAD = 3
-TAN_AHEAD = 4
+TAN_AHEAD = 5
 LAST_TAN_AHEAD = 5
 LAGS = (2, 3, 4, 5, 6)
-SQUARES = ["GGSGSGSG","GGSGSGSG","GGSGSGSG","SGSGSGSG"]
-VECTOR_NORMS = 0
+SQUARES = ["GGSGSGSG","GGSGSGSG","GGSGSGSG","GSGSGSVV"]
+VECTOR_NORMS = 1
 PI_2 = 3.14159 / 2
 EPS = 1e-8
 HUGE = 4096.0
@@ -280,7 +280,7 @@ def tile_memory_t_kernel(tc, key, memory, out):
                     op0=ALU.mult,
                     op1=ALU.add,
                 )
-        unread = keep.tile([P, 1, N], BF16, name="unread")
+        unread = keep.tile([P, 2, N], BF16, name="unread")
         dots = {}
         a_tiles = {}
         b_tiles = {}
@@ -349,15 +349,20 @@ def tile_memory_t_kernel(tc, key, memory, out):
                 out=a_tiles[i][:], in0=b_tiles[i][:], scalar=HUGE, in1=a_tiles[i][:], op0=ALU.min, op1=ALU.mult
             )
 
+        folds = {}
+
+        def fold_max(i):
+            folds[i] = fold_pool.tile([P, BANK], BF16, name="fold")
+            nc.vector.tensor_tensor(
+                out=folds[i][:], in0=a_tiles[i][:, 0:BANK], in1=a_tiles[i][:, BANK:N], op=ALU.max
+            )
+
         def row_max(i, folded=False):
             g, j = group_of[i]
             if folded:
-                fold = fold_pool.tile([P, BANK], BF16, name="fold")
-                nc.vector.tensor_tensor(
-                    out=fold[:], in0=a_tiles[i][:, 0:BANK], in1=a_tiles[i][:, BANK:N], op=ALU.max
-                )
+                fold = folds[i]
                 nc.vector.tensor_scalar(
-                    out=unread[:, 0, 0:BANK],
+                    out=unread[:, i % 2, 0:BANK],
                     in0=fold[:],
                     scalar1=-1.0,
                     scalar2=None,
@@ -367,7 +372,7 @@ def tile_memory_t_kernel(tc, key, memory, out):
                 )
                 return
             nc.vector.tensor_scalar(
-                out=unread[:, 0, :],
+                out=unread[:, i % 2, :],
                 in0=a_tiles[i][:],
                 scalar1=-1.0,
                 scalar2=None,
@@ -503,9 +508,8 @@ def tile_memory_t_kernel(tc, key, memory, out):
                     group_w(last + j, 4)
                 if not is_last:
                     k_step(g + 1, j)
-            for j in range(size):
-                if SQUARES[g][j] == "V" or SQUARES[g][j] == "S" and j == size - 1:
-                    square(here + j, SQUARES[g][j])
+            if SQUARES[g][size - 1] == "S":
+                square(here + size - 1, "S")
             if g == 0:
                 nc.vector.quantize_mx(
                     out=m2_codes[:].bitcast(FP8X4),
@@ -516,6 +520,9 @@ def tile_memory_t_kernel(tc, key, memory, out):
                 quantise_k(g + 1, chunks(GROUP_SIZES[g + 1], 8))
             for j, count in chunks(last_size, 4):
                 quantise_w(g - 1, j, count, 4)
+            for j in range(size):
+                if SQUARES[g][j] == "V":
+                    square(here + j, "V")
             if not is_last:
                 first_matmuls()
             for j in range(min(OUT_BANKS, last_size)):
@@ -540,7 +547,11 @@ def tile_memory_t_kernel(tc, key, memory, out):
                 if j < ahead:
                     tangent(here + j)
                 if 0 < j < ahead:
-                    row_max(here + j - 1, True)
+                    fold_max(here + j - 1)
+                if 1 < j < ahead:
+                    row_max(here + j - 2, True)
+                if j == ahead:
+                    row_max(here + j - 2, True)
                 if not is_last:
                     k_step(g + 1, steps + j)
             if is_last:

@@ -22,15 +22,16 @@ N_BLOCKS = N // P
 N_PASSES = N // K_PASS
 BANK = 512
 HALVES = N // BANK
-DOTS_BANKS = 2
+DOTS_BANKS = 3
 TURN_BANKS = 4
-OUT_BANKS = 2
+OUT_BANKS = 1
 SCALED_AHEAD = 3
 TAN_AHEAD = 5
 LAST_TAN_AHEAD = 5
 LAGS = (2, 3, 4, 5, 6)
-SQUARES = ["GGSGSGSG","GGSGSGSG","GGSGSGSG","GSGSGSVV"]
+SQUARES = ["GGSGSGSG","GGSGGSGG","GGSGGSGG","GSGSGSVV"]
 VECTOR_NORMS = 1
+LAST_ON_GPSIMD = 3
 PI_2 = 3.14159 / 2
 EPS = 1e-8
 HUGE = 4096.0
@@ -100,9 +101,9 @@ def tile_memory_t_kernel(tc, key, memory, out):
         nc.scalar.activation(out=one[:], in_=one[:], func=ACT.Abs_reciprocal_sqrt)
 
         m_sb = keep.tile([P, N_BLOCKS, D], BF16, name="m_sb")
-        for v in range(N_BLOCKS // 2):
-            c, half = divmod(v, 2)
-            nc.sync.dma_start(out=m_sb[:, 2 * v : 2 * v + 2, :], in_=mem_rows[:, c, 2 * half : 2 * half + 2, :])
+        for j, count in ((0, 1), (1, 1), (2, 2), (4, 2), (6, 2)):
+            c, t = divmod(j, PACK)
+            nc.sync.dma_start(out=m_sb[:, j : j + count, :], in_=mem_rows[:, c, t : t + count, :])
 
         k_sb = {}
         loads = list(range(PAIRS))
@@ -391,9 +392,12 @@ def tile_memory_t_kernel(tc, key, memory, out):
                 accum_out=sums[g][:, j : j + 1],
             )
 
-        def normalise(i, engine=nc.gpsimd):
+        def invert_sum(i):
             g, j = group_of[i]
             nc.vector.reciprocal(out=inv_sums[g][:, j : j + 1], in_=sums[g][:, j : j + 1])
+
+        def normalise(i, engine=nc.gpsimd):
+            g, j = group_of[i]
             w_tiles[i] = w_pool.tile([P, N_PASSES, K_PASS], BF16, name="w_tile")
             engine.tensor_scalar(
                 out=w_tiles[i][:].rearrange("p c f -> p (c f)"),
@@ -437,7 +441,7 @@ def tile_memory_t_kernel(tc, key, memory, out):
 
         def second_matmul(i):
             g, j = group_of[i]
-            if g == groups - 1 and j % 4 >= 2:
+            if g == groups - 1 and j % 4 >= OUT_BANKS:
                 out_acc[i] = dots_psum.tile([P, D], F32, name="out_acc", tag="dots")
             else:
                 out_acc[i] = out_psum.tile([P, D], F32, name="out_acc")
@@ -453,9 +457,9 @@ def tile_memory_t_kernel(tc, key, memory, out):
                     stop=(c == N_PASSES - 1),
                 )
 
-        def store(i):
+        def store(i, copy=nc.scalar.copy):
             out_sb = out_pool.tile([P, D], F32, name="out_sb")
-            nc.scalar.copy(out=out_sb[:], in_=out_acc[i][:])
+            copy(out=out_sb[:], in_=out_acc[i][:])
             nc.sync.dma_start(out=out_rows[:, i, :], in_=out_sb[:])
 
 
@@ -568,19 +572,24 @@ def tile_memory_t_kernel(tc, key, memory, out):
                     exponential(here + j)
                 n = j + ahead
                 if 0 < j <= size and not is_last:
-                    normalise(here + j - 1, nc.vector if "GGGGGGGG"[j - 1] == "V" else nc.gpsimd)
+                    invert_sum(here + j - 1)
+                    normalise(here + j - 1)
                 if n < size:
                     tangent(here + n)
                 if n <= size:
                     row_max(here + n - 1)
                 if 0 < j <= size and is_last:
-                    normalise(here + j - 1, nc.vector if "GGGVVVVV"[j - 1] == "V" else nc.gpsimd)
+                    invert_sum(here + j - 1)
+                    if j <= LAST_ON_GPSIMD:
+                        normalise(here + j - 1)
                 if not is_last and j + 1 < last_size:
                     outs(j + 1)
                 n = j - (size - SCALED_AHEAD)
                 if not is_last and 0 <= n < SCALED_AHEAD:
                     scaled_dots(first_of[g + 1] + n)
                 if is_last:
-                    for s, call in enumerate((turn_w, lambda i: group_w(i, 1, nc.scalar.copy if "VVVVSSSS"[i - here] == "S" else nc.vector.tensor_copy), lambda i: quantise_w(g, i - here, 1, 1), second_matmul, store)):
+                    for s, call in enumerate((turn_w, lambda i: group_w(i, 1, nc.scalar.copy if "VVVSVSVS"[i - here] == "S" else nc.vector.tensor_copy), lambda i: quantise_w(g, i - here, 1, 1), second_matmul, lambda i: store(i, nc.scalar.copy if "SSSSSSSS"[i - here] == "S" else nc.vector.tensor_copy))):
                         if 0 <= j - LAGS[s] < size:
                             call(here + j - LAGS[s])
+                    if LAST_ON_GPSIMD < j <= size:
+                        normalise(here + j - 1, nc.vector)

@@ -22,9 +22,9 @@ N_BLOCKS = N // P
 N_PASSES = N // K_PASS
 BANK = 512
 HALVES = N // BANK
-DOTS_BANKS = 3
+DOTS_BANKS = 2
 TURN_BANKS = 4
-OUT_BANKS = 1
+OUT_BANKS = 2
 SCALED_AHEAD = 3
 TAN_AHEAD = 5
 LAST_TAN_AHEAD = 5

@@ -25,11 +25,11 @@ HALVES = N // BANK
 DOTS_BANKS = 2
 TURN_BANKS = 4
 OUT_BANKS = 2
-SCALED_AHEAD = 3
+SCALED_AHEAD = 4
 TAN_AHEAD = 5
 LAST_TAN_AHEAD = 5
 LAGS = (2, 3, 4, 5, 6)
-SQUARES = ["GGSGSGSG","GGSGGSGG","GGSGGSGG","GSGSGSVV"]
+SQUARES = ["GGSGSGSG","GGSGSGSG","GGSGSGSG","GSGSGSVV"]
 VECTOR_NORMS = 1
 LAST_ON_GPSIMD = 3
 PI_2 = 3.14159 / 2
@@ -477,7 +477,7 @@ def tile_memory_t_kernel(tc, key, memory, out):
                         gram_k(q)
                     if step == n + 6:
                         sum_squares_k(q)
-                elif step == n + 5:
+                elif step == n + 6:
                     for a in range(2):
                         j = 2 * n + a
                         sum_squares(k_sb[q][:, a, :], k_sum_sq[g][:, j : j + 1], False)

@@ -17,7 +17,7 @@ K_PASS = P * PACK
 B, N, D = 4096, 1024, 512
 TILES = B // P
 PAIRS = TILES // 2
-GROUP_SIZES = (8, 8, 8, 8)
+GROUP_SIZES = (12, 12, 8)
 N_BLOCKS = N // P
 N_PASSES = N // K_PASS
 BANK = 512
@@ -25,12 +25,13 @@ HALVES = N // BANK
 DOTS_BANKS = 2
 TURN_BANKS = 4
 OUT_BANKS = 2
-SCALED_AHEAD = 4
-TAN_AHEAD = 5
-LAST_TAN_AHEAD = 5
+SCALED_AHEAD = 3
+TAN_AHEAD = 7
+LAST_TAN_AHEAD = 6
 LAGS = (2, 3, 4, 5, 6)
-SQUARES = ["GGSGSGSG","GGSGSGSG","GGSGSGSG","GSGSGSVV"]
+SQUARES = ["GGSGSGSGSGSG", "GGSGSGSGSGSG", "GSGSGSVV"]
 VECTOR_NORMS = 1
+HEAD_TILES = 8
 LAST_ON_GPSIMD = 3
 PI_2 = 3.14159 / 2
 EPS = 1e-8
@@ -49,28 +50,28 @@ def tile_memory_t_kernel(tc, key, memory, out):
         stack.enter_context(tc.manual_schedule())
         keep = stack.enter_context(tc.tile_pool(name="keep", bufs=1))
         k_in = stack.enter_context(tc.tile_pool(name="k_in", bufs=6))
-        k_out = stack.enter_context(tc.tile_pool(name="k_out", bufs=2))
-        grouped_pool = stack.enter_context(tc.tile_pool(name="grouped_pool", bufs=6))
+        k_out = stack.enter_context(tc.tile_pool(name="k_out", bufs=1))
+        grouped_pool = stack.enter_context(tc.tile_pool(name="grouped_pool", bufs=4))
         w_out = stack.enter_context(tc.tile_pool(name="w_out", bufs=1))
         stat = stack.enter_context(tc.tile_pool(name="stat", bufs=1))
         a_pool = stack.enter_context(tc.tile_pool(name="a_pool", bufs=max(GROUP_SIZES) + SCALED_AHEAD))
-        b_pool = stack.enter_context(tc.tile_pool(name="b_pool", bufs=8))
-        w_pool = stack.enter_context(tc.tile_pool(name="w_pool", bufs=9))
+        b_pool = stack.enter_context(tc.tile_pool(name="b_pool", bufs=12))
+        w_pool = stack.enter_context(tc.tile_pool(name="w_pool", bufs=11))
         fold_pool = stack.enter_context(tc.tile_pool(name="fold_pool", bufs=2))
-        out_pool = stack.enter_context(tc.tile_pool(name="out_pool", bufs=5))
+        out_pool = stack.enter_context(tc.tile_pool(name="out_pool", bufs=4))
         dots_psum = stack.enter_context(tc.psum_pool(name="dots_psum", bufs=DOTS_BANKS))
         turn_psum = stack.enter_context(tc.psum_pool(name="turn_psum", bufs=TURN_BANKS))
         out_psum = stack.enter_context(tc.psum_pool(name="out_psum", bufs=OUT_BANKS))
 
         def rough_inverse(sum_sq, width, name):
             rough = stat.tile([P, width], F32, name=name + "_rough")
-            nc.scalar.activation(out=rough[:], in_=sum_sq[:], func=ACT.Abs_reciprocal_sqrt)
+            nc.scalar.activation(out=rough[:], in_=sum_sq, func=ACT.Abs_reciprocal_sqrt)
             return rough
 
         def newton(engine, sum_sq, rough, width, factor, name):
             engine.tensor_scalar_min(out=rough[:], in0=rough[:], scalar1=1.0 / EPS)
             step = stat.tile([P, width], F32, name=name + "_step")
-            engine.tensor_tensor(out=step[:], in0=sum_sq[:], in1=rough[:], op=ALU.mult)
+            engine.tensor_tensor(out=step[:], in0=sum_sq, in1=rough[:], op=ALU.mult)
             engine.tensor_tensor(out=step[:], in0=step[:], in1=rough[:], op=ALU.mult)
             engine.tensor_scalar(
                 out=step[:], in0=step[:], scalar1=-0.5, scalar2=1.5, op0=ALU.mult, op1=ALU.add
@@ -82,6 +83,8 @@ def tile_memory_t_kernel(tc, key, memory, out):
             )
             return fine
 
+        minus_half = keep.tile([P, 8], F32, name="minus_half")
+        nc.gpsimd.memset(minus_half[:], -0.5)
         turned = {}
 
         def turn(name, rows):
@@ -144,7 +147,7 @@ def tile_memory_t_kernel(tc, key, memory, out):
         k_codes = {}
         k_scales = {}
         k_sum_sq = {}
-        k_scale = {}
+        scale_of = {}
         coded = []
         diag = keep.tile([P, 2, P], BF16, name="diag")
 
@@ -225,7 +228,7 @@ def tile_memory_t_kernel(tc, key, memory, out):
 
         for j in range(N_BLOCKS):
             sum_squares(m_sb[:, j, :], m_sum_sq[:, j : j + 1], j < VECTOR_NORMS)
-        m_rough = rough_inverse(m_sum_sq, N_BLOCKS, "m_inv")
+        m_rough = rough_inverse(m_sum_sq[:], N_BLOCKS, "m_inv")
         m1_grouped = [grouped_tile([P, 2, P, 2, PACK]) for h in range(HALVES)]
         m1_codes = keep.tile([P, N], U32, name="m1_codes", align_bytes=64)
         m1_scales = keep.tile([P, N], U8, name="m1_scales", align_bytes=64)
@@ -236,11 +239,11 @@ def tile_memory_t_kernel(tc, key, memory, out):
                 out=m1_grouped[h][:, half, :, :, :].bitcast(F32),
                 in_=turned["m", v][:].rearrange("p e u r -> p r e u"),
             )
-        first_pairs = list(range(GROUP_SIZES[0] // 2))
+        first_pairs = list(range(HEAD_TILES // 2))
         for q in first_pairs:
             turn_k(q)
             group_k(q, None)
-        m_inv = newton(nc.vector, m_sum_sq, m_rough, N_BLOCKS, 1.0, "m_inv")
+        m_inv = newton(nc.vector, m_sum_sq[:], m_rough, N_BLOCKS, 1.0, "m_inv")
         m_inv_all = keep.tile([P, N], F32, name="m_inv_all")
         spreads = []
         for h in range(HALVES):
@@ -259,13 +262,13 @@ def tile_memory_t_kernel(tc, key, memory, out):
                 scales=m1_scales[:, h * BANK : (h + 1) * BANK],
                 in_=m1_grouped[h][:].rearrange("p v r e t -> p (v r e t)"),
             )
-        quantise_k(0, chunks(GROUP_SIZES[0], 8))
+        quantise_k(0, chunks(HEAD_TILES, 8))
         for h in range(HALVES):
             nc.vector.tensor_copy(
                 out=m_inv_all[:, h * BANK : (h + 1) * BANK].rearrange("p (u r e) -> p u r e", u=2, e=2),
                 in_=spreads[h][:].rearrange("p (u e r) -> p u r e", u=2, e=2),
             )
-        for j in range(GROUP_SIZES[0]):
+        for j in range(HEAD_TILES):
             sum_squares(k_sb[j // 2][:, j % 2, :], k_sum_sq[0][:, j : j + 1], j < 0)
 
         m2_grouped = grouped_tile([P, N_PASSES, D, PACK])
@@ -329,7 +332,7 @@ def tile_memory_t_kernel(tc, key, memory, out):
         def sine(i):
             g, j = group_of[i]
             nc.scalar.activation(
-                out=a_tiles[i][:], in_=a_tiles[i][:], func=ACT.Sin, scale=k_scale[g][:, j : j + 1]
+                out=a_tiles[i][:], in_=a_tiles[i][:], func=ACT.Sin, scale=scale_of[i]
             )
 
         def square(i, engine):
@@ -472,7 +475,7 @@ def tile_memory_t_kernel(tc, key, memory, out):
                     turn_k(q)
                 if step == 0 and n == 0:
                     k_sum_sq[g] = stat.tile([P, GROUP_SIZES[g]], F32, name="k_sum_sq%d" % g)
-                if n != 3:
+                if n not in (3, 5):
                     if step == n + 5:
                         gram_k(q)
                     if step == n + 6:
@@ -483,8 +486,40 @@ def tile_memory_t_kernel(tc, key, memory, out):
                         sum_squares(k_sb[q][:, a, :], k_sum_sq[g][:, j : j + 1], False)
 
         first_matmuls()
-        k_rough = rough_inverse(k_sum_sq[0], GROUP_SIZES[0], "k_inv0")
-        k_scale[0] = newton(nc.gpsimd, k_sum_sq[0], k_rough, GROUP_SIZES[0], PI_2, "k_inv0")
+        def inverse_norms(first, sum_sq, count, name):
+            rough = rough_inverse(sum_sq, count, name)
+            scale = newton(nc.gpsimd, sum_sq, rough, count, PI_2, name)
+            for n in range(count):
+                scale_of[first + n] = scale[:, n : n + 1]
+
+        inverse_norms(0, k_sum_sq[0][:, 0:HEAD_TILES], HEAD_TILES, "k_inv0")
+
+        def rest_step(j):
+            pairs = list(range(HEAD_TILES // 2, GROUP_SIZES[0] // 2))
+            count = GROUP_SIZES[0] - HEAD_TILES
+            if j == 0:
+                for q in pairs:
+                    turn_k(q)
+            if j == 1:
+                for q in pairs:
+                    group_k(q)
+            if 1 <= j <= len(pairs):
+                q = pairs[j - 1]
+                for e in range(2):
+                    sum_squares(k_sb[q][:, e, :], k_sum_sq[0][:, 2 * q + e : 2 * q + e + 1], False)
+            if j == 2:
+                quantise_k(0, [(HEAD_TILES + a, b) for a, b in chunks(count, 8)])
+            if j == len(pairs) + 1:
+                rest = stat.tile([P, count], F32, name="k_rest")
+                nc.gpsimd.tensor_tensor(
+                    out=rest[:], in0=k_sum_sq[0][:, HEAD_TILES:], in1=minus_half[:, 0:count], op=ALU.pow
+                )
+                nc.gpsimd.tensor_scalar(
+                    out=rest[:], in0=rest[:], scalar1=1.0 / EPS, scalar2=PI_2, op0=ALU.min, op1=ALU.mult
+                )
+                for n in range(count):
+                    scale_of[HEAD_TILES + n] = rest[:, n : n + 1]
+
         for i in range(SCALED_AHEAD):
             scaled_dots(i)
 
@@ -504,6 +539,8 @@ def tile_memory_t_kernel(tc, key, memory, out):
                         square(here + j, "G")
                     if j > 0 and SQUARES[g][j - 1] == "S":
                         square(here + j - 1, "S")
+                if g == 0 and HEAD_TILES < size:
+                    rest_step(j)
                 if j < last_size:
                     turn_w(last + j)
                 if j + SCALED_AHEAD < size:
@@ -546,7 +583,7 @@ def tile_memory_t_kernel(tc, key, memory, out):
                 inverse_cosine(here + j)
                 if j + 4 < size and SQUARES[g][j + 4] == "R":
                     square(here + j + 4, "S")
-                if (is_last or j >= size - 1) and j < last_size:
+                if is_last or j >= size - 1:
                     outs(j if is_last else j - size + 1)
                 if j < ahead:
                     tangent(here + j)
@@ -562,10 +599,7 @@ def tile_memory_t_kernel(tc, key, memory, out):
                 for j in range(size, last_size):
                     outs(j)
             if not is_last:
-                k_rough = rough_inverse(k_sum_sq[g + 1], GROUP_SIZES[g + 1], "k_inv%d" % (g + 1))
-                k_scale[g + 1] = newton(
-                    nc.gpsimd, k_sum_sq[g + 1], k_rough, GROUP_SIZES[g + 1], PI_2, "k_inv%d" % (g + 1)
-                )
+                inverse_norms(first_of[g + 1], k_sum_sq[g + 1][:], GROUP_SIZES[g + 1], "k_inv%d" % (g + 1))
 
             for j in range(size + 1 if not is_last else size + LAGS[-1]):
                 if j < size:
@@ -588,7 +622,7 @@ def tile_memory_t_kernel(tc, key, memory, out):
                 if not is_last and 0 <= n < SCALED_AHEAD:
                     scaled_dots(first_of[g + 1] + n)
                 if is_last:
-                    for s, call in enumerate((turn_w, lambda i: group_w(i, 1, nc.scalar.copy if "VVVSVSVS"[i - here] == "S" else nc.vector.tensor_copy), lambda i: quantise_w(g, i - here, 1, 1), second_matmul, lambda i: store(i, nc.scalar.copy if "SSSSSSSS"[i - here] == "S" else nc.vector.tensor_copy))):
+                    for s, call in enumerate((turn_w, lambda i: group_w(i, 1, nc.scalar.copy if ("V" * (size - 5) + "SVSVS")[i - here] == "S" else nc.vector.tensor_copy), lambda i: quantise_w(g, i - here, 1, 1), second_matmul, lambda i: store(i, nc.scalar.copy if "SSSSSSSS"[i - here] == "S" else nc.vector.tensor_copy))):
                         if 0 <= j - LAGS[s] < size:
                             call(here + j - LAGS[s])
                     if LAST_ON_GPSIMD < j <= size:

from contextlib import ExitStack

import concourse.mybir as mybir
from concourse.masks import make_identity

F32 = mybir.dt.float32
BF16 = mybir.dt.bfloat16
U32 = mybir.dt.uint32
U8 = mybir.dt.uint8
FP8X4 = mybir.dt.float8_e4m3fn_x4
ACT = mybir.ActivationFunctionType
ALU = mybir.AluOpType

P = 128
PACK = 4
K_PASS = P * PACK
B, N, D = 4096, 1024, 512
TILES = B // P
PAIRS = TILES // 2
GROUP_SIZES = (12, 12, 8)
N_BLOCKS = N // P
N_PASSES = N // K_PASS
BANK = 512
HALVES = N // BANK
DOTS_BANKS = 2
TURN_BANKS = 4
OUT_BANKS = 2
SCALED_AHEAD = 3
TAN_AHEAD = 7
LAST_TAN_AHEAD = 6
LAGS = (2, 3, 4, 5, 6)
SQUARES = ["GGSGSGSGSGSG", "GGSGSGSGSGSG", "GSGSGSVV"]
VECTOR_NORMS = 1
HEAD_TILES = 8
LAST_ON_GPSIMD = 3
PI_2 = 3.14159 / 2
EPS = 1e-8
HUGE = 4096.0

FLOPS = 2 * B * N * D * 2


def tile_memory_t_kernel(tc, key, memory, out):
    nc = tc.nc
    key_rows = key.rearrange("(p i) c h w -> p i (c h w)", i=TILES)
    out_rows = out.rearrange("(p i) c h w -> p i (c h w)", i=TILES)
    mem_rows = memory.rearrange("(c p t) a h w -> p c t (a h w)", c=N_PASSES, t=PACK)

    with ExitStack() as stack:
        stack.enter_context(tc.manual_schedule())
        keep = stack.enter_context(tc.tile_pool(name="keep", bufs=1))
        k_in = stack.enter_context(tc.tile_pool(name="k_in", bufs=6))
        k_out = stack.enter_context(tc.tile_pool(name="k_out", bufs=1))
        grouped_pool = stack.enter_context(tc.tile_pool(name="grouped_pool", bufs=4))
        w_out = stack.enter_context(tc.tile_pool(name="w_out", bufs=1))
        stat = stack.enter_context(tc.tile_pool(name="stat", bufs=1))
        a_pool = stack.enter_context(tc.tile_pool(name="a_pool", bufs=max(GROUP_SIZES) + SCALED_AHEAD))
        b_pool = stack.enter_context(tc.tile_pool(name="b_pool", bufs=12))
        w_pool = stack.enter_context(tc.tile_pool(name="w_pool", bufs=11))
        fold_pool = stack.enter_context(tc.tile_pool(name="fold_pool", bufs=2))
        out_pool = stack.enter_context(tc.tile_pool(name="out_pool", bufs=4))
        dots_psum = stack.enter_context(tc.psum_pool(name="dots_psum", bufs=DOTS_BANKS))
        turn_psum = stack.enter_context(tc.psum_pool(name="turn_psum", bufs=TURN_BANKS))
        out_psum = stack.enter_context(tc.psum_pool(name="out_psum", bufs=OUT_BANKS))

        def rough_inverse(sum_sq, width, name):
            rough = stat.tile([P, width], F32, name=name + "_rough")
            nc.scalar.activation(out=rough[:], in_=sum_sq, func=ACT.Abs_reciprocal_sqrt)
            return rough

        def newton(engine, sum_sq, rough, width, factor, name):
            engine.tensor_scalar_min(out=rough[:], in0=rough[:], scalar1=1.0 / EPS)
            step = stat.tile([P, width], F32, name=name + "_step")
            engine.tensor_tensor(out=step[:], in0=sum_sq, in1=rough[:], op=ALU.mult)
            engine.tensor_tensor(out=step[:], in0=step[:], in1=rough[:], op=ALU.mult)
            engine.tensor_scalar(
                out=step[:], in0=step[:], scalar1=-0.5, scalar2=1.5, op0=ALU.mult, op1=ALU.add
            )
            fine = stat.tile([P, width], F32, name=name + "_fine")
            engine.tensor_tensor(out=fine[:], in0=rough[:], in1=step[:], op=ALU.mult)
            engine.tensor_scalar(
                out=fine[:], in0=fine[:], scalar1=1.0 / EPS, scalar2=factor, op0=ALU.min, op1=ALU.mult
            )
            return fine

        minus_half = keep.tile([P, 8], F32, name="minus_half")
        nc.gpsimd.memset(minus_half[:], -0.5)
        turned = {}

        def turn(name, rows):
            words = rows.bitcast(F32)
            turned[name] = turn_psum.tile([P, 2, 2, P], F32, name="turned", tag="turned")
            for a in range(2):
                for u in range(2):
                    nc.tensor.transpose(
                        out=turned[name][:, a, u, :], in_=words[:, a, u * P : (u + 1) * P], identity=ident_f32[:]
                    )

        def grouped_tile(shape):
            return grouped_pool.tile(shape, BF16, name="grouped", tag="grouped", align_bytes=64)

        one = keep.tile([P, 1], F32, name="one")
        nc.vector.memset(one[:], 1.0)
        nc.scalar.activation(out=one[:], in_=one[:], func=ACT.Abs_reciprocal_sqrt)

        m_sb = keep.tile([P, N_BLOCKS, D], BF16, name="m_sb")
        for j, count in ((0, 1), (1, 1), (2, 2), (4, 2), (6, 2)):
            c, t = divmod(j, PACK)
            nc.sync.dma_start(out=m_sb[:, j : j + count, :], in_=mem_rows[:, c, t : t + count, :])

        k_sb = {}
        loads = list(range(PAIRS))

        def load_k():
            if loads:
                q = loads[0]
                k_sb[q] = k_in.tile([P, 2, D], BF16, name="k_sb")
                nc.sync.dma_start(out=k_sb[q][:], in_=key_rows[:, 2 * q : 2 * q + 2, :])
                loads.remove(q)

        for q in range(6):
            load_k()

        ident_f32 = keep.tile([P, P], F32, name="ident_f32")
        make_identity(nc, ident_f32[:])

        groups = len(GROUP_SIZES)
        group_of = {}
        first_of = []
        for g, size in enumerate(GROUP_SIZES):
            first_of.append(len(group_of))
            for j in range(size):
                group_of[first_of[g] + j] = (g, j)

        def chunks(size, largest):
            runs = []
            j = 0
            while j < size:
                count = largest
                while j + count > size:
                    count //= 2
                runs.append((j, count))
                j += count
            return runs

        k_chunk = {}
        k_codes = {}
        k_scales = {}
        k_sum_sq = {}
        scale_of = {}
        coded = []
        diag = keep.tile([P, 2, P], BF16, name="diag")

        def k_place(i):
            g, j = group_of[i]
            for first, count in chunks(GROUP_SIZES[g], 8):
                if first <= j < first + count:
                    if (g, first) not in k_chunk:
                        k_chunk[g, first] = grouped_tile([P, 8, P, PACK])
                    return k_chunk[g, first], j - first

        def turn_k(q):
            turn(("k", q), k_sb[q][:])
            load_k()

        def group_k(q, engine=None):
            rows, j = k_place(2 * q)
            (engine or nc.vector.tensor_copy)(
                out=rows[:, j : j + 2, :, :].bitcast(F32),
                in_=turned["k", q][:].rearrange("p a u r -> p a r u"),
            )

        def quantise_k(g, runs):
            size = GROUP_SIZES[g]
            if g not in k_codes:
                k_codes[g] = k_out.tile([P, max(GROUP_SIZES) * P], U32, name="k_codes", align_bytes=64)
                k_scales[g] = k_out.tile([P, max(GROUP_SIZES) * P], U8, name="k_scales", align_bytes=64)
            for j, count in runs:
                rows, at = k_place(first_of[g] + j)
                nc.vector.quantize_mx(
                    out=k_codes[g][:, j * P : (j + count) * P].bitcast(FP8X4),
                    scales=k_scales[g][:, j * P : (j + count) * P],
                    in_=rows[:, at : at + count, :, :].rearrange("p a r t -> p (a r t)"),
                )
                for n in range(j, j + count):
                    coded.append(first_of[g] + n)

        gram = {}

        def gram_k(q):
            gram[q] = turn_psum.tile([P, 2, P], F32, name="gram", tag="turned")
            rows, j = k_place(2 * q)
            for a in range(2):
                for t in range(PACK):
                    nc.tensor.matmul(
                        out=gram[q][:, a, :],
                        lhsT=rows[:, j + a, :, t],
                        rhs=rows[:, j + a, :, t],
                        start=(t == 0),
                        stop=(t == PACK - 1),
                    )

        def sum_squares_k(q):
            for a in range(2):
                g, j = group_of[2 * q + a]
                nc.vector.scalar_tensor_tensor(
                    out=diag[:, a, :],
                    in0=gram[q][:, a, :],
                    scalar=1.0,
                    in1=ident_f32[:],
                    op0=ALU.mult,
                    op1=ALU.mult,
                    accum_out=k_sum_sq[g][:, j : j + 1],
                )

        squares_pool = stack.enter_context(tc.tile_pool(name="squares_pool", bufs=3))
        m_sum_sq = keep.tile([P, N_BLOCKS], F32, name="m_sum_sq")
        k_sum_sq[0] = stat.tile([P, GROUP_SIZES[0]], F32, name="k_sum_sq0")

        def sum_squares(rows, accum, on_vector):
            squares = squares_pool.tile([P, D], BF16, name="squares")
            if on_vector:
                nc.vector.scalar_tensor_tensor(
                    out=squares[:], in0=rows, scalar=1.0, in1=rows, op0=ALU.mult, op1=ALU.mult, accum_out=accum
                )
            else:
                nc.scalar.activation(out=squares[:], in_=rows, func=ACT.Square, accum_out=accum)

        for j in range(N_BLOCKS):
            sum_squares(m_sb[:, j, :], m_sum_sq[:, j : j + 1], j < VECTOR_NORMS)
        m_rough = rough_inverse(m_sum_sq[:], N_BLOCKS, "m_inv")
        m1_grouped = [grouped_tile([P, 2, P, 2, PACK]) for h in range(HALVES)]
        m1_codes = keep.tile([P, N], U32, name="m1_codes", align_bytes=64)
        m1_scales = keep.tile([P, N], U8, name="m1_scales", align_bytes=64)
        for v in range(N_BLOCKS // 2):
            turn(("m", v), m_sb[:, 2 * v : 2 * v + 2, :])
            h, half = divmod(v, 2)
            nc.vector.tensor_copy(
                out=m1_grouped[h][:, half, :, :, :].bitcast(F32),
                in_=turned["m", v][:].rearrange("p e u r -> p r e u"),
            )
        first_pairs = list(range(HEAD_TILES // 2))
        for q in first_pairs:
            turn_k(q)
            group_k(q, None)
        m_inv = newton(nc.vector, m_sum_sq[:], m_rough, N_BLOCKS, 1.0, "m_inv")
        m_inv_all = keep.tile([P, N], F32, name="m_inv_all")
        spreads = []
        for h in range(HALVES):
            spread = dots_psum.tile([P, BANK], F32, name="spread", tag="dots")
            for a in range(BANK // P):
                j = h * (BANK // P) + a
                nc.tensor.transpose(
                    out=spread[:, a * P : (a + 1) * P],
                    in_=m_inv[:, j : j + 1].to_broadcast([P, P]),
                    identity=ident_f32[:],
                )
            spreads.append(spread)
        for h in range(HALVES):
            nc.vector.quantize_mx(
                out=m1_codes[:, h * BANK : (h + 1) * BANK].bitcast(FP8X4),
                scales=m1_scales[:, h * BANK : (h + 1) * BANK],
                in_=m1_grouped[h][:].rearrange("p v r e t -> p (v r e t)"),
            )
        quantise_k(0, chunks(HEAD_TILES, 8))
        for h in range(HALVES):
            nc.vector.tensor_copy(
                out=m_inv_all[:, h * BANK : (h + 1) * BANK].rearrange("p (u r e) -> p u r e", u=2, e=2),
                in_=spreads[h][:].rearrange("p (u e r) -> p u r e", u=2, e=2),
            )
        for j in range(HEAD_TILES):
            sum_squares(k_sb[j // 2][:, j % 2, :], k_sum_sq[0][:, j : j + 1], j < 0)

        m2_grouped = grouped_tile([P, N_PASSES, D, PACK])
        m2_codes = keep.tile([P, N_PASSES * D], U32, name="m2_codes", align_bytes=64)
        m2_scales = keep.tile([P, N_PASSES * D], U8, name="m2_scales", align_bytes=64)
        for c in range(N_PASSES):
            for d in range(0, D, P):
                nc.gpsimd.tensor_scalar(
                    out=m2_grouped[:, c, d : d + P, :],
                    in0=m_sb[:, c * PACK : (c + 1) * PACK, d : d + P].rearrange("p t d -> p d t"),
                    scalar1=1.0,
                    scalar2=0.0,
                    op0=ALU.mult,
                    op1=ALU.add,
                )
        unread = keep.tile([P, 2, N], BF16, name="unread")
        dots = {}
        a_tiles = {}
        b_tiles = {}
        neg_max = {}
        sums = {}
        inv_sums = {}
        w_tiles = {}
        w_grouped = {}
        w_codes = {}
        w_scales = {}
        out_acc = {}
        dots_order = [(i, h) for i in range(TILES) for h in range(HALVES)]
        scaled_order = list(dots_order)

        def first_matmuls():
            while dots_order and len(dots_order) > len(scaled_order) - DOTS_BANKS:
                i, h = dots_order[0]
                g, j = group_of[i]
                if i not in coded:
                    return
                dots[i, h] = dots_psum.tile([P, BANK], F32, name="dots", tag="dots")
                nc.tensor.matmul_mx(
                    out=dots[i, h][:],
                    lhsT=k_codes[g][:, j * P : (j + 1) * P].bitcast(FP8X4),
                    lhsT_scale=k_scales[g][:, j * P : (j + 1) * P],
                    rhs=m1_codes[:, h * BANK : (h + 1) * BANK].bitcast(FP8X4),
                    rhs_scale=m1_scales[:, h * BANK : (h + 1) * BANK],
                    start=True,
                    stop=True,
                )
                dots_order.remove((i, h))

        def scaled_dots(i):
            a_tiles[i] = a_pool.tile([P, N], F32, name="a_tile")
            for h in range(HALVES):
                nc.vector.tensor_tensor(
                    out=a_tiles[i][:, h * BANK : (h + 1) * BANK],
                    in0=dots[i, h][:],
                    in1=m_inv_all[:, h * BANK : (h + 1) * BANK],
                    op=ALU.mult,
                )
                scaled_order.remove((i, h))
                first_matmuls()

        def sine(i):
            g, j = group_of[i]
            nc.scalar.activation(
                out=a_tiles[i][:], in_=a_tiles[i][:], func=ACT.Sin, scale=scale_of[i]
            )

        def square(i, engine):
            b_tiles[i] = b_pool.tile([P, N], F32, name="b_tile")
            if engine == "S":
                nc.scalar.activation(out=b_tiles[i][:], in_=a_tiles[i][:], func=ACT.Square)
            else:
                e = nc.gpsimd if engine == "G" else nc.vector
                e.tensor_tensor(out=b_tiles[i][:], in0=a_tiles[i][:], in1=a_tiles[i][:], op=ALU.mult)

        def inverse_cosine(i):
            nc.scalar.activation(
                out=b_tiles[i][:], in_=b_tiles[i][:], func=ACT.Abs_reciprocal_sqrt, scale=-1.0, bias=1.0
            )

        def tangent(i):
            nc.vector.scalar_tensor_tensor(
                out=a_tiles[i][:], in0=b_tiles[i][:], scalar=HUGE, in1=a_tiles[i][:], op0=ALU.min, op1=ALU.mult
            )

        folds = {}

        def fold_max(i):
            folds[i] = fold_pool.tile([P, BANK], BF16, name="fold")
            nc.vector.tensor_tensor(
                out=folds[i][:], in0=a_tiles[i][:, 0:BANK], in1=a_tiles[i][:, BANK:N], op=ALU.max
            )

        def row_max(i, folded=False):
            g, j = group_of[i]
            if folded:
                fold = folds[i]
                nc.vector.tensor_scalar(
                    out=unread[:, i % 2, 0:BANK],
                    in0=fold[:],
                    scalar1=-1.0,
                    scalar2=None,
                    op0=ALU.mult,
                    op1=ALU.min,
                    accum_out=neg_max[g][:, j : j + 1],
                )
                return
            nc.vector.tensor_scalar(
                out=unread[:, i % 2, :],
                in0=a_tiles[i][:],
                scalar1=-1.0,
                scalar2=None,
                op0=ALU.mult,
                op1=ALU.min,
                accum_out=neg_max[g][:, j : j + 1],
            )

        def exponential(i):
            g, j = group_of[i]
            nc.scalar.activation(
                out=a_tiles[i][:],
                in_=a_tiles[i][:],
                func=ACT.Exp,
                bias=neg_max[g][:, j : j + 1],
                accum_out=sums[g][:, j : j + 1],
            )

        def invert_sum(i):
            g, j = group_of[i]
            nc.vector.reciprocal(out=inv_sums[g][:, j : j + 1], in_=sums[g][:, j : j + 1])

        def normalise(i, engine=nc.gpsimd):
            g, j = group_of[i]
            w_tiles[i] = w_pool.tile([P, N_PASSES, K_PASS], BF16, name="w_tile")
            engine.tensor_scalar(
                out=w_tiles[i][:].rearrange("p c f -> p (c f)"),
                in0=a_tiles[i][:],
                scalar1=inv_sums[g][:, j : j + 1],
                scalar2=0.0,
                op0=ALU.mult,
                op1=ALU.add,
            )

        def turn_w(i):
            turn(("w", i), w_tiles[i][:])

        w_chunk = {}

        def w_place(i, largest):
            g, j = group_of[i]
            for first, count in chunks(GROUP_SIZES[g], largest):
                if first <= j < first + count:
                    if (g, first) not in w_chunk:
                        w_chunk[g, first] = grouped_tile([P, 4, N_PASSES, P, PACK])
                    return w_chunk[g, first], j - first

        def group_w(i, largest, engine=None):
            rows, j = w_place(i, largest)
            (engine or nc.vector.tensor_copy)(
                out=rows[:, j, :, :, :].bitcast(F32), in_=turned["w", i][:].rearrange("p c u r -> p c r u")
            )

        def quantise_w(g, j, count, largest):
            if j == 0:
                w_codes[g] = w_out.tile([P, max(GROUP_SIZES) * N_PASSES * P], U32, name="w_codes", align_bytes=64)
                w_scales[g] = w_out.tile([P, max(GROUP_SIZES) * N_PASSES * P], U8, name="w_scales", align_bytes=64)
            rows, at = w_place(first_of[g] + j, largest)
            lo, hi = j * N_PASSES * P, (j + count) * N_PASSES * P
            nc.vector.quantize_mx(
                out=w_codes[g][:, lo:hi].bitcast(FP8X4),
                scales=w_scales[g][:, lo:hi],
                in_=rows[:, at : at + count, :, :, :].rearrange("p j c r t -> p (j c r t)"),
            )

        def second_matmul(i):
            g, j = group_of[i]
            if g == groups - 1 and j % 4 >= OUT_BANKS:
                out_acc[i] = dots_psum.tile([P, D], F32, name="out_acc", tag="dots")
            else:
                out_acc[i] = out_psum.tile([P, D], F32, name="out_acc")
            for c in range(N_PASSES):
                lo = (j * N_PASSES + c) * P
                nc.tensor.matmul_mx(
                    out=out_acc[i][:],
                    lhsT=w_codes[g][:, lo : lo + P].bitcast(FP8X4),
                    lhsT_scale=w_scales[g][:, lo : lo + P],
                    rhs=m2_codes[:, c * D : (c + 1) * D].bitcast(FP8X4),
                    rhs_scale=m2_scales[:, c * D : (c + 1) * D],
                    start=(c == 0),
                    stop=(c == N_PASSES - 1),
                )

        def store(i, copy=nc.scalar.copy):
            out_sb = out_pool.tile([P, D], F32, name="out_sb")
            copy(out=out_sb[:], in_=out_acc[i][:])
            nc.sync.dma_start(out=out_rows[:, i, :], in_=out_sb[:])


        def k_step(g, step):
            pairs = list(range(first_of[g] // 2, (first_of[g] + GROUP_SIZES[g]) // 2))
            for n, q in enumerate(pairs):
                if step == n + 1:
                    group_k(q)
                if step == n:
                    turn_k(q)
                if step == 0 and n == 0:
                    k_sum_sq[g] = stat.tile([P, GROUP_SIZES[g]], F32, name="k_sum_sq%d" % g)
                if n not in (3, 5):
                    if step == n + 5:
                        gram_k(q)
                    if step == n + 6:
                        sum_squares_k(q)
                elif step == n + 6:
                    for a in range(2):
                        j = 2 * n + a
                        sum_squares(k_sb[q][:, a, :], k_sum_sq[g][:, j : j + 1], False)

        first_matmuls()
        def inverse_norms(first, sum_sq, count, name):
            rough = rough_inverse(sum_sq, count, name)
            scale = newton(nc.gpsimd, sum_sq, rough, count, PI_2, name)
            for n in range(count):
                scale_of[first + n] = scale[:, n : n + 1]

        inverse_norms(0, k_sum_sq[0][:, 0:HEAD_TILES], HEAD_TILES, "k_inv0")

        def rest_step(j):
            pairs = list(range(HEAD_TILES // 2, GROUP_SIZES[0] // 2))
            count = GROUP_SIZES[0] - HEAD_TILES
            if j == 0:
                for q in pairs:
                    turn_k(q)
            if j == 1:
                for q in pairs:
                    group_k(q)
            if 1 <= j <= len(pairs):
                q = pairs[j - 1]
                for e in range(2):
                    sum_squares(k_sb[q][:, e, :], k_sum_sq[0][:, 2 * q + e : 2 * q + e + 1], False)
            if j == 2:
                quantise_k(0, [(HEAD_TILES + a, b) for a, b in chunks(count, 8)])
            if j == len(pairs) + 1:
                rest = stat.tile([P, count], F32, name="k_rest")
                nc.gpsimd.tensor_tensor(
                    out=rest[:], in0=k_sum_sq[0][:, HEAD_TILES:], in1=minus_half[:, 0:count], op=ALU.pow
                )
                nc.gpsimd.tensor_scalar(
                    out=rest[:], in0=rest[:], scalar1=1.0 / EPS, scalar2=PI_2, op0=ALU.min, op1=ALU.mult
                )
                for n in range(count):
                    scale_of[HEAD_TILES + n] = rest[:, n : n + 1]

        for i in range(SCALED_AHEAD):
            scaled_dots(i)

        for g in range(groups):
            size = GROUP_SIZES[g]
            here = first_of[g]
            last = first_of[g - 1] if g > 0 else None
            last_size = GROUP_SIZES[g - 1] if g > 0 else 0
            is_last = g + 1 == groups

            w_left = list(range(last_size))
            steps = max(size, last_size)
            for j in range(steps):
                if j < size:
                    sine(here + j)
                    if SQUARES[g][j] == "G":
                        square(here + j, "G")
                    if j > 0 and SQUARES[g][j - 1] == "S":
                        square(here + j - 1, "S")
                if g == 0 and HEAD_TILES < size:
                    rest_step(j)
                if j < last_size:
                    turn_w(last + j)
                if j + SCALED_AHEAD < size:
                    scaled_dots(here + j + SCALED_AHEAD)
                if j < last_size:
                    group_w(last + j, 4)
                if not is_last:
                    k_step(g + 1, j)
            if SQUARES[g][size - 1] == "S":
                square(here + size - 1, "S")
            if g == 0:
                nc.vector.quantize_mx(
                    out=m2_codes[:].bitcast(FP8X4),
                    scales=m2_scales[:],
                    in_=m2_grouped[:].rearrange("p c d t -> p (c d t)"),
                )
            if not is_last:
                quantise_k(g + 1, chunks(GROUP_SIZES[g + 1], 8))
            for j, count in chunks(last_size, 4):
                quantise_w(g - 1, j, count, 4)
            for j in range(size):
                if SQUARES[g][j] == "V":
                    square(here + j, "V")
            if not is_last:
                first_matmuls()
            for j in range(min(OUT_BANKS, last_size)):
                second_matmul(last + j)

            def outs(j):
                if j < last_size:
                    store(last + j)
                    if j + OUT_BANKS < last_size:
                        second_matmul(last + j + OUT_BANKS)

            neg_max[g] = stat.tile([P, size], F32, name="neg_max%d" % g)
            sums[g] = stat.tile([P, size], F32, name="sums%d" % g)
            inv_sums[g] = stat.tile([P, size], F32, name="inv_sums%d" % g)
            ahead = LAST_TAN_AHEAD if is_last else TAN_AHEAD
            for j in range(size):
                inverse_cosine(here + j)
                if j + 4 < size and SQUARES[g][j + 4] == "R":
                    square(here + j + 4, "S")
                if is_last or j >= size - 1:
                    outs(j if is_last else j - size + 1)
                if j < ahead:
                    tangent(here + j)
                if 0 < j < ahead:
                    fold_max(here + j - 1)
                if 1 < j < ahead:
                    row_max(here + j - 2, True)
                if j == ahead:
                    row_max(here + j - 2, True)
                if not is_last:
                    k_step(g + 1, steps + j)
            if is_last:
                for j in range(size, last_size):
                    outs(j)
            if not is_last:
                inverse_norms(first_of[g + 1], k_sum_sq[g + 1][:], GROUP_SIZES[g + 1], "k_inv%d" % (g + 1))

            for j in range(size + 1 if not is_last else size + LAGS[-1]):
                if j < size:
                    exponential(here + j)
                n = j + ahead
                if 0 < j <= size and not is_last:
                    invert_sum(here + j - 1)
                    normalise(here + j - 1)
                if n < size:
                    tangent(here + n)
                if n <= size:
                    row_max(here + n - 1)
                if 0 < j <= size and is_last:
                    invert_sum(here + j - 1)
                    if j <= LAST_ON_GPSIMD:
                        normalise(here + j - 1)
                if not is_last and j + 1 < last_size:
                    outs(j + 1)
                n = j - (size - SCALED_AHEAD)
                if not is_last and 0 <= n < SCALED_AHEAD:
                    scaled_dots(first_of[g + 1] + n)
                if is_last:
                    for s, call in enumerate((turn_w, lambda i: group_w(i, 1, nc.scalar.copy if ("V" * (size - 5) + "SVSVS")[i - here] == "S" else nc.vector.tensor_copy), lambda i: quantise_w(g, i - here, 1, 1), second_matmul, lambda i: store(i, nc.scalar.copy if "SSSSSSSS"[i - here] == "S" else nc.vector.tensor_copy))):
                        if 0 <= j - LAGS[s] < size:
                            call(here + j - LAGS[s])
                    if LAST_ON_GPSIMD < j <= size:
                        normalise(here + j - 1, nc.vector)
